import numpy as np
import ml_dtypes


def mxq(x, axis, fmt="e4m3"):
    dtype, down = {"e4m3": (ml_dtypes.float8_e4m3fn, 7), "e5m2": (ml_dtypes.float8_e5m2, 14)}[fmt]
    v = np.moveaxis(np.asarray(x, np.float32).astype(ml_dtypes.bfloat16).astype(np.float64), axis, -1)
    blocks = v.reshape(v.shape[:-1] + (-1, 32))
    amax = np.abs(blocks).max(-1, keepdims=True)
    byte = np.maximum(np.where(amax > 0, np.frexp(amax)[1] - 1 + 127, 0) - down, 1)
    scale = np.exp2(byte - 127.0)
    codes = (blocks / scale).astype(np.float32).astype(dtype).astype(np.float64)
    return np.moveaxis((codes * scale).reshape(v.shape), -1, axis)


WIDE = False


def mx_kscale(k):
    if not WIDE:
        return np.ones(k)
    levels = np.array([10, -10, 5, -5, 0])
    a = np.random.permutation(np.resize(levels, k // 512 * 4)).reshape(k // 512, 4)
    idx = np.arange(k)
    return np.exp2(a[idx // 512, idx % 128 // 32])


BF16 = ml_dtypes.bfloat16


def bf(x):
    return np.asarray(x, np.float32).astype(BF16)


def f64(x):
    return np.asarray(x).astype(np.float64)


B, N, F_IN, F_HID, F_OUT = 4, 1024, 512, 512, 512


def normalize_adj(adj):
    colsum = adj.sum(axis=1)
    safe = np.where(colsum > 0, colsum, 1.0)
    r = np.where(colsum > 0, safe ** -0.5, 0.0)
    return r[:, :, None] * adj.transpose(0, 2, 1) * r[:, None, :]


def setup_inputs():
    t = mx_kscale(F_HID)
    keep = np.random.random((B, 1, N)) >= 0.05
    level = np.random.standard_normal((B, 1, F_HID)) * 2.5
    spread = np.random.standard_normal((B, N, F_HID)) * 0.15 * np.sqrt(N)
    return {"adj": bf(np.random.random((B, N, N)) * keep),
            "msg": bf((level + spread) * t),
            "b2": bf(np.random.standard_normal(F_HID) * 0.2 * t),
            "W3": bf(np.random.standard_normal((F_HID, F_OUT)) * 2.0 / np.sqrt(F_HID) / t[:, None])}


def reference(adj, msg, b2, W3):
    a = normalize_adj(f64(adj))
    x = np.maximum((mxq(a, 2, "e4m3") @ mxq(f64(msg), 1, "e4m3")) + f64(b2), 0.0)
    return mxq(x, 2, "e4m3") @ mxq(f64(W3), 0, "e4m3")

@@ -1,0 +1,293 @@
+from contextlib import ExitStack
+
+import concourse.mybir as mybir
+from concourse.masks import make_identity
+
+BF16 = mybir.dt.bfloat16
+F32 = mybir.dt.float32
+U32 = mybir.dt.uint32
+U8 = mybir.dt.uint8
+FP8X4 = mybir.dt.float8_e4m3fn_x4
+ALU = mybir.AluOpType
+ACT = mybir.ActivationFunctionType
+
+GRAPHS = 4
+NODES = 1024
+HIDDEN = 512
+OUT = 512
+P = 128
+PACK = 4
+K_PASS = P * PACK
+PASSES = NODES // K_PASS
+NODE_TILES = NODES // P
+ROUND = 512
+PARTS = NODES // ROUND
+ROUNDS = GRAPHS * PARTS
+RUN = 4
+SUM_COPIES = 8
+SIDE_LEAD = 5
+
+FLOPS = 2 * GRAPHS * NODES * NODES * HIDDEN + 2 * GRAPHS * NODES * HIDDEN * OUT
+
+
+def tile_gcn_pb_kernel(tc, adj, msg, b2, W3, out):
+    nc = tc.nc
+
+    def regroup(copy, grouped, rows):
+        copy(
+            out=grouped.rearrange("p (w i) t -> p w t i", i=RUN),
+            in_=rows.rearrange("p t (w i) -> p w t i", i=RUN),
+        )
+
+    def quantise(codes, scales, grouped):
+        nc.vector.quantize_mx(
+            out=codes.bitcast(FP8X4), scales=scales, in_=grouped.rearrange("p w t -> p (w t)")
+        )
+
+    with ExitStack() as ctx:
+        ctx.enter_context(tc.manual_schedule())
+        const = ctx.enter_context(tc.tile_pool(name="const", bufs=1))
+        inputs = ctx.enter_context(tc.tile_pool(name="inputs", bufs=GRAPHS))
+        small = ctx.enter_context(tc.tile_pool(name="small", bufs=2))
+        side_pool = ctx.enter_context(tc.tile_pool(name="side_pool", bufs=SIDE_LEAD))
+        stage = ctx.enter_context(tc.tile_pool(name="stage", bufs=2))
+        operand = ctx.enter_context(tc.tile_pool(name="operand", bufs=2 * PASSES))
+        store = ctx.enter_context(tc.tile_pool(name="store", bufs=6))
+        psum_sum = ctx.enter_context(tc.psum_pool(name="psum_sum", bufs=1))
+        psum_r = ctx.enter_context(tc.psum_pool(name="psum_r", bufs=2))
+        psum_x = ctx.enter_context(tc.psum_pool(name="psum_x", bufs=3))
+        psum_out = ctx.enter_context(tc.psum_pool(name="psum_out", bufs=2))
+
+        ones = const.tile([P, SUM_COPIES], BF16)
+        nc.vector.memset(ones[:], 1.0)
+        minus_half = const.tile([P, NODE_TILES], F32)
+        nc.vector.memset(minus_half[:], -0.5)
+        identity = const.tile([P, P], F32)
+        make_identity(nc, identity[:])
+
+        raw_adj = {}
+        raw_msg = {}
+
+        def load_adj(g):
+            raw_adj[g] = inputs.tile([P, PASSES, PACK, NODES], BF16, name="raw_adj")
+            rows = adj[g].rearrange("(c t p) i -> c p t i", t=PACK, p=P)
+            for c in range(PASSES):
+                nc.sync.dma_start(out=raw_adj[g][:, c], in_=rows[c])
+
+        def load_msg(g):
+            raw_msg[g] = inputs.tile([P, PASSES, PACK, HIDDEN], BF16, name="raw_msg")
+            nc.sync.dma_start(
+                out=raw_msg[g][:].rearrange("p c t f -> p (c t) f"),
+                in_=msg[g].rearrange("(a p) f -> p a f", p=P),
+            )
+
+        load_adj(0)
+        load_msg(0)
+        raw_w3 = const.tile([P, PACK, OUT], BF16)
+        nc.sync.dma_start(out=raw_w3[:], in_=W3.rearrange("(t p) o -> p t o", p=P))
+        raw_b2 = const.tile([P, PACK], BF16)
+        with nc.allow_non_contiguous_dma(reason="512 bias values, one to a partition and word slot"):
+            nc.sync.dma_start(out=raw_b2[:], in_=b2.rearrange("(t p) -> p t", p=P))
+        for g in range(1, GRAPHS):
+            load_msg(g)
+            load_adj(g)
+
+        w_codes = const.tile([P, OUT], U32, align_bytes=64)
+        w_scales = const.tile([P, OUT], U8, align_bytes=64)
+        m_codes = {}
+        m_scales = {}
+        side = []
+        for g in range(GRAPHS):
+            m_codes[g] = inputs.tile([P, PASSES, HIDDEN], U32, name="m_codes", align_bytes=64)
+            m_scales[g] = inputs.tile([P, PASSES, HIDDEN], U8, name="m_scales", align_bytes=64)
+            for c in range(PASSES):
+                side.append((raw_msg[g][:, c], m_codes[g][:, c, :], m_scales[g][:, c, :]))
+            if g == 0:
+                side.append((raw_w3[:], w_codes[:], w_scales[:]))
+        side_grouped = {}
+
+        def regroup_side(n):
+            if n < len(side):
+                side_grouped[n] = side_pool.tile([P, HIDDEN, PACK], BF16, name="side_grouped", align_bytes=64)
+                regroup(nc.scalar.copy, side_grouped[n][:], side[n][0])
+
+        def quantise_side(n):
+            if n < len(side):
+                quantise(side[n][1], side[n][2], side_grouped[n][:])
+
+        partial = {}
+        r_of = {}
+        r_row = {}
+        scaled = {}
+        a_grouped = {}
+        a_operand = {}
+        x_rows = {}
+        x_grouped = {}
+        x_operand = {}
+
+        def column_sums(g):
+            if g >= GRAPHS:
+                return
+            partial[g] = psum_sum.tile([P, NODE_TILES, NODE_TILES, SUM_COPIES], F32, name="partial")
+            for c in range(PASSES):
+                for t in range(PACK):
+                    for b in range(NODE_TILES):
+                        nc.tensor.matmul(
+                            out=partial[g][:, c * PACK + t, b, :],
+                            lhsT=raw_adj[g][:, c, t, b * P : (b + 1) * P],
+                            rhs=ones[:],
+                            start=True,
+                            stop=True,
+                        )
+
+        def node_scales(g):
+            if g >= GRAPHS:
+                return
+            colsum = small.tile([P, NODE_TILES], F32)
+            nc.vector.tensor_reduce(
+                out=colsum[:],
+                in_=partial[g][:, :, :, 0].rearrange("p a b -> p b a"),
+                axis=mybir.AxisListType.X,
+                op=ALU.add,
+            )
+            empty = small.tile([P, NODE_TILES], F32)
+            nc.gpsimd.tensor_single_scalar(out=empty[:], in_=colsum[:], scalar=0.0, op=ALU.is_le)
+            safe = small.tile([P, NODE_TILES], F32)
+            nc.gpsimd.tensor_tensor(out=safe[:], in0=colsum[:], in1=empty[:], op=ALU.add)
+            root = small.tile([P, NODE_TILES], F32)
+            nc.gpsimd.tensor_tensor(out=root[:], in0=safe[:], in1=minus_half[:], op=ALU.pow)
+            r_of[g] = small.tile([P, NODE_TILES], F32, name="r")
+            nc.gpsimd.tensor_tensor(out=r_of[g][:], in0=root[:], in1=empty[:], op=ALU.subtract)
+
+        def spread_scales(k):
+            if k >= ROUNDS:
+                return
+            g, part = divmod(k, PARTS)
+            r_row[k] = psum_r.tile([P, ROUND], F32, name="r_row")
+            for q in range(ROUND // P):
+                b = part * (ROUND // P) + q
+                nc.tensor.matmul(
+                    out=r_row[k][:, q * P : (q + 1) * P],
+                    lhsT=r_of[g][:, b : b + 1].to_broadcast([P, P]),
+                    rhs=identity[:],
+                    start=True,
+                    stop=True,
+                )
+
+        def scale_rows(k, c):
+            if k >= ROUNDS:
+                return
+            g, part = divmod(k, PARTS)
+            scaled[k, c] = stage.tile([P, PACK, ROUND], BF16, name="scaled")
+            for t in range(PACK):
+                a = c * PACK + t
+                nc.vector.scalar_tensor_tensor(
+                    out=scaled[k, c][:, t, :],
+                    in0=raw_adj[g][:, c, t, part * ROUND : (part + 1) * ROUND],
+                    scalar=r_of[g][:, a : a + 1],
+                    in1=r_row[k][:],
+                    op0=ALU.mult,
+                    op1=ALU.mult,
+                )
+
+        def regroup_adjacency(k, c):
+            if k >= ROUNDS:
+                return
+            a_grouped[k, c] = stage.tile([P, ROUND, PACK], BF16, name="a_grouped", align_bytes=64)
+            regroup(nc.vector.tensor_copy, a_grouped[k, c][:], scaled[k, c][:])
+
+        def quantise_adjacency(k, c):
+            if k >= ROUNDS:
+                return
+            a_codes = operand.tile([P, ROUND], U32, align_bytes=64)
+            a_scales = operand.tile([P, ROUND], U8, align_bytes=64)
+            quantise(a_codes[:], a_scales[:], a_grouped[k, c][:])
+            a_operand[k, c] = (a_codes, a_scales)
+
+        def hidden_layer(k):
+            if not 0 <= k < ROUNDS:
+                return
+            g = k // PARTS
+            x_rows[k] = stage.tile([P, PACK, ROUND], BF16, name="x_rows")
+            for t in range(PACK):
+                features = slice(t * P, (t + 1) * P)
+                x_sum = psum_x.tile([P, ROUND], F32)
+                for c in range(PASSES):
+                    a_codes, a_scales = a_operand[k, c]
+                    nc.tensor.matmul_mx(
+                        out=x_sum[:],
+                        lhsT=m_codes[g][:, c, features].bitcast(FP8X4),
+                        lhsT_scale=m_scales[g][:, c, features],
+                        rhs=a_codes[:].bitcast(FP8X4),
+                        rhs_scale=a_scales[:],
+                        start=(c == 0),
+                        stop=(c == PASSES - 1),
+                    )
+                nc.scalar.activation(
+                    out=x_rows[k][:, t, :], in_=x_sum[:], func=ACT.Relu, bias=bias[:, t : t + 1], scale=1.0
+                )
+
+        def regroup_hidden(k):
+            if not 0 <= k < ROUNDS:
+                return
+            x_grouped[k] = stage.tile([P, ROUND, PACK], BF16, name="x_grouped", align_bytes=64)
+            regroup(nc.scalar.copy, x_grouped[k][:], x_rows[k][:])
+
+        def quantise_hidden(k):
+            if not 0 <= k < ROUNDS:
+                return
+            x_codes = operand.tile([P, ROUND], U32, align_bytes=64)
+            x_scales = operand.tile([P, ROUND], U8, align_bytes=64)
+            quantise(x_codes[:], x_scales[:], x_grouped[k][:])
+            x_operand[k] = (x_codes, x_scales)
+
+        def project(k):
+            if not 0 <= k < ROUNDS:
+                return
+            g, part = divmod(k, PARTS)
+            x_codes, x_scales = x_operand[k]
+            for n in range(ROUND // P):
+                nodes = slice(n * P, (n + 1) * P)
+                product = psum_out.tile([P, OUT], F32)
+                nc.tensor.matmul_mx(
+                    out=product[:],
+                    lhsT=x_codes[:, nodes].bitcast(FP8X4),
+                    lhsT_scale=x_scales[:, nodes],
+                    rhs=w_codes[:].bitcast(FP8X4),
+                    rhs_scale=w_scales[:],
+                    start=True,
+                    stop=True,
+                )
+                result = store.tile([P, OUT], F32)
+                nc.scalar.copy(out=result[:], in_=product[:])
+                first = part * ROUND + n * P
+                nc.sync.dma_start(out=out[g, first : first + P, :], in_=result[:])
+
+        column_sums(0)
+        node_scales(0)
+        spread_scales(0)
+        bias = const.tile([P, PACK], F32)
+        nc.vector.tensor_copy(out=bias[:], in_=raw_b2[:])
+        for n in range(SIDE_LEAD):
+            regroup_side(n)
+
+        for k in range(ROUNDS + 2):
+            g, part = divmod(k, PARTS)
+            scale_rows(k, 0)
+            project(k - 2)
+            if part == 1:
+                node_scales(g + 1)
+            regroup_adjacency(k, 0)
+            hidden_layer(k - 1)
+            scale_rows(k, 1)
+            quantise_adjacency(k, 0)
+            regroup_hidden(k - 1)
+            spread_scales(k + 1)
+            regroup_adjacency(k, 1)
+            if part == 0:
+                column_sums(g + 1)
+            quantise_hidden(k - 1)
+            quantise_adjacency(k, 1)
+            for n in range(0 if k == 0 else SIDE_LEAD + k - 1, SIDE_LEAD + k):
+                quantise_side(n)
+            regroup_side(SIDE_LEAD + k)

@@ -21,17 +21,28 @@ K_PASS = P * PACK
 PASSES = NODES // K_PASS
 NODE_TILES = NODES // P
 ROUND = 512
-PARTS = NODES // ROUND
-ROUNDS = GRAPHS * PARTS
 RUN = 4
 SUM_COPIES = 8
-SIDE_LEAD = 5
 
 FLOPS = 2 * GRAPHS * NODES * NODES * HIDDEN + 2 * GRAPHS * NODES * HIDDEN * OUT
 
 
 def tile_gcn_pb_kernel(tc, adj, msg, b2, W3, out):
     nc = tc.nc
+
+    rounds = []
+    for g in range(GRAPHS):
+        for first in range(0, NODES, ROUND):
+            rounds.append((g, first, ROUND))
+    g, first, width = rounds.pop()
+    while width > P:
+        width //= 2
+        rounds.append((g, first, width))
+        first += width
+    rounds.append((g, first, width))
+
+    def round_starts_at(k, node):
+        return k < len(rounds) and rounds[k][1] == node
 
     def regroup(copy, grouped, rows):
         copy(
@@ -49,8 +60,8 @@ def tile_gcn_pb_kernel(tc, adj, msg, b2, W3, out):
         const = ctx.enter_context(tc.tile_pool(name="const", bufs=1))
         inputs = ctx.enter_context(tc.tile_pool(name="inputs", bufs=GRAPHS))
         small = ctx.enter_context(tc.tile_pool(name="small", bufs=2))
-        side_pool = ctx.enter_context(tc.tile_pool(name="side_pool", bufs=SIDE_LEAD))
         stage = ctx.enter_context(tc.tile_pool(name="stage", bufs=2))
+        handover = ctx.enter_context(tc.tile_pool(name="handover", bufs=1))
         operand = ctx.enter_context(tc.tile_pool(name="operand", bufs=2 * PASSES))
         store = ctx.enter_context(tc.tile_pool(name="store", bufs=6))
         psum_sum = ctx.enter_context(tc.psum_pool(name="psum_sum", bufs=1))
@@ -60,8 +71,9 @@ def tile_gcn_pb_kernel(tc, adj, msg, b2, W3, out):
 
         ones = const.tile([P, SUM_COPIES], BF16)
         nc.vector.memset(ones[:], 1.0)
-        minus_half = const.tile([P, NODE_TILES], F32)
-        nc.vector.memset(minus_half[:], -0.5)
+        warm = const.tile([P, 1], F32)
+        nc.vector.memset(warm[:], 1.0)
+        nc.scalar.sqrt(out=warm[:], in_=warm[:])
         identity = const.tile([P, P], F32)
         make_identity(nc, identity[:])
 
@@ -89,33 +101,16 @@ def tile_gcn_pb_kernel(tc, adj, msg, b2, W3, out):
         with nc.allow_non_contiguous_dma(reason="512 bias values, one to a partition and word slot"):
             nc.sync.dma_start(out=raw_b2[:], in_=b2.rearrange("(t p) -> p t", p=P))
         for g in range(1, GRAPHS):
-            load_msg(g)
             load_adj(g)
+            load_msg(g)
 
-        w_codes = const.tile([P, OUT], U32, align_bytes=64)
-        w_scales = const.tile([P, OUT], U8, align_bytes=64)
+        m_grouped = {}
         m_codes = {}
         m_scales = {}
-        side = []
-        for g in range(GRAPHS):
-            m_codes[g] = inputs.tile([P, PASSES, HIDDEN], U32, name="m_codes", align_bytes=64)
-            m_scales[g] = inputs.tile([P, PASSES, HIDDEN], U8, name="m_scales", align_bytes=64)
-            for c in range(PASSES):
-                side.append((raw_msg[g][:, c], m_codes[g][:, c, :], m_scales[g][:, c, :]))
-            if g == 0:
-                side.append((raw_w3[:], w_codes[:], w_scales[:]))
-        side_grouped = {}
-
-        def regroup_side(n):
-            if n < len(side):
-                side_grouped[n] = side_pool.tile([P, HIDDEN, PACK], BF16, name="side_grouped", align_bytes=64)
-                regroup(nc.scalar.copy, side_grouped[n][:], side[n][0])
-
-        def quantise_side(n):
-            if n < len(side):
-                quantise(side[n][1], side[n][2], side_grouped[n][:])
-
         partial = {}
+        empty = {}
+        safe = {}
+        root = {}
         r_of = {}
         r_row = {}
         scaled = {}
@@ -124,6 +119,21 @@ def tile_gcn_pb_kernel(tc, adj, msg, b2, W3, out):
         x_rows = {}
         x_grouped = {}
         x_operand = {}
+
+        def regroup_messages(g, copy):
+            if g >= GRAPHS:
+                return
+            for c in range(PASSES):
+                m_grouped[g, c] = stage.tile([P, HIDDEN, PACK], BF16, name="m_grouped", align_bytes=64)
+                regroup(copy, m_grouped[g, c][:], raw_msg[g][:, c])
+
+        def quantise_messages(g):
+            if g >= GRAPHS:
+                return
+            m_codes[g] = inputs.tile([P, PASSES, HIDDEN], U32, name="m_codes", align_bytes=64)
+            m_scales[g] = inputs.tile([P, PASSES, HIDDEN], U8, name="m_scales", align_bytes=64)
+            for c in range(PASSES):
+                quantise(m_codes[g][:, c, :], m_scales[g][:, c, :], m_grouped[g, c][:])
 
         def column_sums(g):
             if g >= GRAPHS:
@@ -140,7 +150,7 @@ def tile_gcn_pb_kernel(tc, adj, msg, b2, W3, out):
                             stop=True,
                         )
 
-        def node_scales(g):
+        def column_sum_roots(g):
             if g >= GRAPHS:
                 return
             colsum = small.tile([P, NODE_TILES], F32)
@@ -150,22 +160,38 @@ def tile_gcn_pb_kernel(tc, adj, msg, b2, W3, out):
                 axis=mybir.AxisListType.X,
                 op=ALU.add,
             )
-            empty = small.tile([P, NODE_TILES], F32)
-            nc.gpsimd.tensor_single_scalar(out=empty[:], in_=colsum[:], scalar=0.0, op=ALU.is_le)
-            safe = small.tile([P, NODE_TILES], F32)
-            nc.gpsimd.tensor_tensor(out=safe[:], in0=colsum[:], in1=empty[:], op=ALU.add)
-            root = small.tile([P, NODE_TILES], F32)
-            nc.gpsimd.tensor_tensor(out=root[:], in0=safe[:], in1=minus_half[:], op=ALU.pow)
+            empty[g] = small.tile([P, NODE_TILES], F32, name="empty")
+            nc.vector.tensor_single_scalar(out=empty[g][:], in_=colsum[:], scalar=0.0, op=ALU.is_le)
+            safe[g] = small.tile([P, NODE_TILES], F32, name="safe")
+            nc.vector.tensor_tensor(out=safe[g][:], in0=colsum[:], in1=empty[g][:], op=ALU.max)
+            root[g] = small.tile([P, NODE_TILES], F32, name="root")
+            nc.scalar.sqrt(out=root[g][:], in_=safe[g][:])
+
+        def node_scales(g):
+            if g >= GRAPHS:
+                return
+            guess = small.tile([P, NODE_TILES], F32)
+            nc.vector.reciprocal(out=guess[:], in_=root[g][:])
+            once = small.tile([P, NODE_TILES], F32)
+            nc.vector.tensor_tensor(out=once[:], in0=guess[:], in1=safe[g][:], op=ALU.mult)
+            twice = small.tile([P, NODE_TILES], F32)
+            nc.vector.tensor_tensor(out=twice[:], in0=once[:], in1=guess[:], op=ALU.mult)
+            factor = small.tile([P, NODE_TILES], F32)
+            nc.vector.tensor_scalar(
+                out=factor[:], in0=twice[:], scalar1=-0.5, scalar2=1.5, op0=ALU.mult, op1=ALU.add
+            )
+            refined = small.tile([P, NODE_TILES], F32)
+            nc.vector.tensor_tensor(out=refined[:], in0=guess[:], in1=factor[:], op=ALU.mult)
             r_of[g] = small.tile([P, NODE_TILES], F32, name="r")
-            nc.gpsimd.tensor_tensor(out=r_of[g][:], in0=root[:], in1=empty[:], op=ALU.subtract)
+            nc.vector.tensor_tensor(out=r_of[g][:], in0=refined[:], in1=empty[g][:], op=ALU.subtract)
 
         def spread_scales(k):
-            if k >= ROUNDS:
+            if k >= len(rounds):
                 return
-            g, part = divmod(k, PARTS)
-            r_row[k] = psum_r.tile([P, ROUND], F32, name="r_row")
-            for q in range(ROUND // P):
-                b = part * (ROUND // P) + q
+            g, first, width = rounds[k]
+            r_row[k] = psum_r.tile([P, width], F32, name="r_row")
+            for q in range(width // P):
+                b = first // P + q
                 nc.tensor.matmul(
                     out=r_row[k][:, q * P : (q + 1) * P],
                     lhsT=r_of[g][:, b : b + 1].to_broadcast([P, P]),
@@ -175,15 +201,15 @@ def tile_gcn_pb_kernel(tc, adj, msg, b2, W3, out):
                 )
 
         def scale_rows(k, c):
-            if k >= ROUNDS:
+            if k >= len(rounds):
                 return
-            g, part = divmod(k, PARTS)
-            scaled[k, c] = stage.tile([P, PACK, ROUND], BF16, name="scaled")
+            g, first, width = rounds[k]
+            scaled[k, c] = stage.tile([P, PACK, width], BF16, name="scaled")
             for t in range(PACK):
                 a = c * PACK + t
                 nc.vector.scalar_tensor_tensor(
                     out=scaled[k, c][:, t, :],
-                    in0=raw_adj[g][:, c, t, part * ROUND : (part + 1) * ROUND],
+                    in0=raw_adj[g][:, c, t, first : first + width],
                     scalar=r_of[g][:, a : a + 1],
                     in1=r_row[k][:],
                     op0=ALU.mult,
@@ -191,27 +217,36 @@ def tile_gcn_pb_kernel(tc, adj, msg, b2, W3, out):
                 )
 
         def regroup_adjacency(k, c):
-            if k >= ROUNDS:
+            if k >= len(rounds):
                 return
-            a_grouped[k, c] = stage.tile([P, ROUND, PACK], BF16, name="a_grouped", align_bytes=64)
-            regroup(nc.vector.tensor_copy, a_grouped[k, c][:], scaled[k, c][:])
+            width = rounds[k][2]
+            a_grouped[k, c] = handover.tile([P, width, PACK], BF16, name="a_grouped", align_bytes=64)
+            nc.gpsimd.tensor_scalar(
+                out=a_grouped[k, c][:],
+                in0=scaled[k, c][:].rearrange("p t w -> p w t"),
+                scalar1=1.0,
+                scalar2=0.0,
+                op0=ALU.mult,
+                op1=ALU.add,
+            )
 
         def quantise_adjacency(k, c):
-            if k >= ROUNDS:
+            if not 0 <= k < len(rounds):
                 return
-            a_codes = operand.tile([P, ROUND], U32, align_bytes=64)
-            a_scales = operand.tile([P, ROUND], U8, align_bytes=64)
+            width = rounds[k][2]
+            a_codes = operand.tile([P, width], U32, align_bytes=64)
+            a_scales = operand.tile([P, width], U8, align_bytes=64)
             quantise(a_codes[:], a_scales[:], a_grouped[k, c][:])
             a_operand[k, c] = (a_codes, a_scales)
 
         def hidden_layer(k):
-            if not 0 <= k < ROUNDS:
+            if not 0 <= k < len(rounds):
                 return
-            g = k // PARTS
-            x_rows[k] = stage.tile([P, PACK, ROUND], BF16, name="x_rows")
+            g, first, width = rounds[k]
+            x_rows[k] = stage.tile([P, PACK, width], BF16, name="x_rows")
             for t in range(PACK):
                 features = slice(t * P, (t + 1) * P)
-                x_sum = psum_x.tile([P, ROUND], F32)
+                x_sum = psum_x.tile([P, width], F32)
                 for c in range(PASSES):
                     a_codes, a_scales = a_operand[k, c]
                     nc.tensor.matmul_mx(
@@ -228,25 +263,27 @@ def tile_gcn_pb_kernel(tc, adj, msg, b2, W3, out):
                 )
 
         def regroup_hidden(k):
-            if not 0 <= k < ROUNDS:
+            if not 0 <= k < len(rounds):
                 return
-            x_grouped[k] = stage.tile([P, ROUND, PACK], BF16, name="x_grouped", align_bytes=64)
+            width = rounds[k][2]
+            x_grouped[k] = stage.tile([P, width, PACK], BF16, name="x_grouped", align_bytes=64)
             regroup(nc.scalar.copy, x_grouped[k][:], x_rows[k][:])
 
         def quantise_hidden(k):
-            if not 0 <= k < ROUNDS:
+            if not 0 <= k < len(rounds):
                 return
-            x_codes = operand.tile([P, ROUND], U32, align_bytes=64)
-            x_scales = operand.tile([P, ROUND], U8, align_bytes=64)
+            width = rounds[k][2]
+            x_codes = operand.tile([P, width], U32, align_bytes=64)
+            x_scales = operand.tile([P, width], U8, align_bytes=64)
             quantise(x_codes[:], x_scales[:], x_grouped[k][:])
             x_operand[k] = (x_codes, x_scales)
 
         def project(k):
-            if not 0 <= k < ROUNDS:
+            if not 0 <= k < len(rounds):
                 return
-            g, part = divmod(k, PARTS)
+            g, first, width = rounds[k]
             x_codes, x_scales = x_operand[k]
-            for n in range(ROUND // P):
+            for n in range(width // P):
                 nodes = slice(n * P, (n + 1) * P)
                 product = psum_out.tile([P, OUT], F32)
                 nc.tensor.matmul_mx(
@@ -260,34 +297,40 @@ def tile_gcn_pb_kernel(tc, adj, msg, b2, W3, out):
                 )
                 result = store.tile([P, OUT], F32)
                 nc.scalar.copy(out=result[:], in_=product[:])
-                first = part * ROUND + n * P
-                nc.sync.dma_start(out=out[g, first : first + P, :], in_=result[:])
+                nc.sync.dma_start(out=out[g, first + n * P : first + (n + 1) * P, :], in_=result[:])
 
         column_sums(0)
+        column_sum_roots(0)
         node_scales(0)
         spread_scales(0)
+        column_sums(1)
+        regroup_messages(0, nc.scalar.copy)
+        w_grouped = const.tile([P, OUT, PACK], BF16, align_bytes=64)
+        w_codes = const.tile([P, OUT], U32, align_bytes=64)
+        w_scales = const.tile([P, OUT], U8, align_bytes=64)
+        regroup(nc.scalar.copy, w_grouped[:], raw_w3[:])
         bias = const.tile([P, PACK], F32)
         nc.vector.tensor_copy(out=bias[:], in_=raw_b2[:])
-        for n in range(SIDE_LEAD):
-            regroup_side(n)
 
-        for k in range(ROUNDS + 2):
-            g, part = divmod(k, PARTS)
+        for k in range(len(rounds) + 2):
+            spread_scales(k + 1)
             scale_rows(k, 0)
-            project(k - 2)
-            if part == 1:
-                node_scales(g + 1)
+            quantise_messages(k)
+            if round_starts_at(k, 0):
+                column_sum_roots(rounds[k][0] + 1)
+            quantise_adjacency(k - 1, 1)
             regroup_adjacency(k, 0)
             hidden_layer(k - 1)
             scale_rows(k, 1)
-            quantise_adjacency(k, 0)
             regroup_hidden(k - 1)
-            spread_scales(k + 1)
+            if k == 0:
+                quantise(w_codes[:], w_scales[:], w_grouped[:])
+            if round_starts_at(k, 0):
+                node_scales(rounds[k][0] + 1)
+            quantise_hidden(k - 2)
+            quantise_adjacency(k, 0)
             regroup_adjacency(k, 1)
-            if part == 0:
-                column_sums(g + 1)
-            quantise_hidden(k - 1)
-            quantise_adjacency(k, 1)
-            for n in range(0 if k == 0 else SIDE_LEAD + k - 1, SIDE_LEAD + k):
-                quantise_side(n)
-            regroup_side(SIDE_LEAD + k)
+            project(k - 2)
+            if round_starts_at(k, ROUND):
+                column_sums(rounds[k][0] + 2)
+            regroup_messages(k + 1, nc.scalar.copy)

@@ -22,6 +22,8 @@ PASSES = NODES // K_PASS
 NODE_TILES = NODES // P
 ROUND = 512
 RUN = 4
+SIDE_LEAD = 7
+SIDE_PER_TURN = 3
 SUM_COPIES = 8
 
 FLOPS = 2 * GRAPHS * NODES * NODES * HIDDEN + 2 * GRAPHS * NODES * HIDDEN * OUT
@@ -60,8 +62,8 @@ def tile_gcn_pb_kernel(tc, adj, msg, b2, W3, out):
         const = ctx.enter_context(tc.tile_pool(name="const", bufs=1))
         inputs = ctx.enter_context(tc.tile_pool(name="inputs", bufs=GRAPHS))
         small = ctx.enter_context(tc.tile_pool(name="small", bufs=2))
+        side_pool = ctx.enter_context(tc.tile_pool(name="side_pool", bufs=SIDE_LEAD))
         stage = ctx.enter_context(tc.tile_pool(name="stage", bufs=2))
-        handover = ctx.enter_context(tc.tile_pool(name="handover", bufs=1))
         operand = ctx.enter_context(tc.tile_pool(name="operand", bufs=2 * PASSES))
         store = ctx.enter_context(tc.tile_pool(name="store", bufs=6))
         psum_sum = ctx.enter_context(tc.psum_pool(name="psum_sum", bufs=1))
@@ -71,9 +73,8 @@ def tile_gcn_pb_kernel(tc, adj, msg, b2, W3, out):
 
         ones = const.tile([P, SUM_COPIES], BF16)
         nc.vector.memset(ones[:], 1.0)
-        warm = const.tile([P, 1], F32)
-        nc.vector.memset(warm[:], 1.0)
-        nc.scalar.sqrt(out=warm[:], in_=warm[:])
+        minus_half = const.tile([P, NODE_TILES], F32)
+        nc.vector.memset(minus_half[:], -0.5)
         identity = const.tile([P, P], F32)
         make_identity(nc, identity[:])
 
@@ -100,17 +101,27 @@ def tile_gcn_pb_kernel(tc, adj, msg, b2, W3, out):
         raw_b2 = const.tile([P, PACK], BF16)
         with nc.allow_non_contiguous_dma(reason="512 bias values, one to a partition and word slot"):
             nc.sync.dma_start(out=raw_b2[:], in_=b2.rearrange("(t p) -> p t", p=P))
-        for g in range(1, GRAPHS):
-            load_adj(g)
-            load_msg(g)
+        load_msg(1)
+        load_adj(1)
+        load_msg(2)
+        load_msg(3)
+        load_adj(2)
+        load_adj(3)
 
-        m_grouped = {}
+        w_codes = const.tile([P, OUT], U32, align_bytes=64)
+        w_scales = const.tile([P, OUT], U8, align_bytes=64)
         m_codes = {}
         m_scales = {}
+        side = []
+        for g in range(GRAPHS):
+            m_codes[g] = inputs.tile([P, PASSES, HIDDEN], U32, name="m_codes", align_bytes=64)
+            m_scales[g] = inputs.tile([P, PASSES, HIDDEN], U8, name="m_scales", align_bytes=64)
+            for c in range(PASSES):
+                side.append((raw_msg[g][:, c], m_codes[g][:, c, :], m_scales[g][:, c, :]))
+            if g == 0:
+                side.append((raw_w3[:], w_codes[:], w_scales[:]))
+        side_grouped = {}
         partial = {}
-        empty = {}
-        safe = {}
-        root = {}
         r_of = {}
         r_row = {}
         scaled = {}
@@ -120,20 +131,14 @@ def tile_gcn_pb_kernel(tc, adj, msg, b2, W3, out):
         x_grouped = {}
         x_operand = {}
 
-        def regroup_messages(g, copy):
-            if g >= GRAPHS:
-                return
-            for c in range(PASSES):
-                m_grouped[g, c] = stage.tile([P, HIDDEN, PACK], BF16, name="m_grouped", align_bytes=64)
-                regroup(copy, m_grouped[g, c][:], raw_msg[g][:, c])
+        def regroup_side(n):
+            if n < len(side):
+                side_grouped[n] = side_pool.tile([P, HIDDEN, PACK], BF16, name="side_grouped", align_bytes=64)
+                regroup(nc.scalar.copy, side_grouped[n][:], side[n][0])
 
-        def quantise_messages(g):
-            if g >= GRAPHS:
-                return
-            m_codes[g] = inputs.tile([P, PASSES, HIDDEN], U32, name="m_codes", align_bytes=64)
-            m_scales[g] = inputs.tile([P, PASSES, HIDDEN], U8, name="m_scales", align_bytes=64)
-            for c in range(PASSES):
-                quantise(m_codes[g][:, c, :], m_scales[g][:, c, :], m_grouped[g, c][:])
+        def quantise_side(n):
+            if n < len(side):
+                quantise(side[n][1], side[n][2], side_grouped[n][:])
 
         def column_sums(g):
             if g >= GRAPHS:
@@ -150,7 +155,7 @@ def tile_gcn_pb_kernel(tc, adj, msg, b2, W3, out):
                             stop=True,
                         )
 
-        def column_sum_roots(g):
+        def node_scales(g):
             if g >= GRAPHS:
                 return
             colsum = small.tile([P, NODE_TILES], F32)
@@ -160,30 +165,14 @@ def tile_gcn_pb_kernel(tc, adj, msg, b2, W3, out):
                 axis=mybir.AxisListType.X,
                 op=ALU.add,
             )
-            empty[g] = small.tile([P, NODE_TILES], F32, name="empty")
-            nc.vector.tensor_single_scalar(out=empty[g][:], in_=colsum[:], scalar=0.0, op=ALU.is_le)
-            safe[g] = small.tile([P, NODE_TILES], F32, name="safe")
-            nc.vector.tensor_tensor(out=safe[g][:], in0=colsum[:], in1=empty[g][:], op=ALU.max)
-            root[g] = small.tile([P, NODE_TILES], F32, name="root")
-            nc.scalar.sqrt(out=root[g][:], in_=safe[g][:])
-
-        def node_scales(g):
-            if g >= GRAPHS:
-                return
-            guess = small.tile([P, NODE_TILES], F32)
-            nc.vector.reciprocal(out=guess[:], in_=root[g][:])
-            once = small.tile([P, NODE_TILES], F32)
-            nc.vector.tensor_tensor(out=once[:], in0=guess[:], in1=safe[g][:], op=ALU.mult)
-            twice = small.tile([P, NODE_TILES], F32)
-            nc.vector.tensor_tensor(out=twice[:], in0=once[:], in1=guess[:], op=ALU.mult)
-            factor = small.tile([P, NODE_TILES], F32)
-            nc.vector.tensor_scalar(
-                out=factor[:], in0=twice[:], scalar1=-0.5, scalar2=1.5, op0=ALU.mult, op1=ALU.add
-            )
-            refined = small.tile([P, NODE_TILES], F32)
-            nc.vector.tensor_tensor(out=refined[:], in0=guess[:], in1=factor[:], op=ALU.mult)
+            empty = small.tile([P, NODE_TILES], F32)
+            nc.gpsimd.tensor_single_scalar(out=empty[:], in_=colsum[:], scalar=0.0, op=ALU.is_le)
+            safe = small.tile([P, NODE_TILES], F32)
+            nc.gpsimd.tensor_tensor(out=safe[:], in0=colsum[:], in1=empty[:], op=ALU.add)
+            root = small.tile([P, NODE_TILES], F32)
+            nc.gpsimd.tensor_tensor(out=root[:], in0=safe[:], in1=minus_half[:], op=ALU.pow)
             r_of[g] = small.tile([P, NODE_TILES], F32, name="r")
-            nc.vector.tensor_tensor(out=r_of[g][:], in0=refined[:], in1=empty[g][:], op=ALU.subtract)
+            nc.gpsimd.tensor_tensor(out=r_of[g][:], in0=root[:], in1=empty[:], op=ALU.subtract)
 
         def spread_scales(k):
             if k >= len(rounds):
@@ -220,18 +209,11 @@ def tile_gcn_pb_kernel(tc, adj, msg, b2, W3, out):
             if k >= len(rounds):
                 return
             width = rounds[k][2]
-            a_grouped[k, c] = handover.tile([P, width, PACK], BF16, name="a_grouped", align_bytes=64)
-            nc.gpsimd.tensor_scalar(
-                out=a_grouped[k, c][:],
-                in0=scaled[k, c][:].rearrange("p t w -> p w t"),
-                scalar1=1.0,
-                scalar2=0.0,
-                op0=ALU.mult,
-                op1=ALU.add,
-            )
+            a_grouped[k, c] = stage.tile([P, width, PACK], BF16, name="a_grouped", align_bytes=64)
+            regroup(nc.vector.tensor_copy, a_grouped[k, c][:], scaled[k, c][:])
 
         def quantise_adjacency(k, c):
-            if not 0 <= k < len(rounds):
+            if k >= len(rounds):
                 return
             width = rounds[k][2]
             a_codes = operand.tile([P, width], U32, align_bytes=64)
@@ -300,37 +282,30 @@ def tile_gcn_pb_kernel(tc, adj, msg, b2, W3, out):
                 nc.sync.dma_start(out=out[g, first + n * P : first + (n + 1) * P, :], in_=result[:])
 
         column_sums(0)
-        column_sum_roots(0)
         node_scales(0)
         spread_scales(0)
         column_sums(1)
-        regroup_messages(0, nc.scalar.copy)
-        w_grouped = const.tile([P, OUT, PACK], BF16, align_bytes=64)
-        w_codes = const.tile([P, OUT], U32, align_bytes=64)
-        w_scales = const.tile([P, OUT], U8, align_bytes=64)
-        regroup(nc.scalar.copy, w_grouped[:], raw_w3[:])
         bias = const.tile([P, PACK], F32)
         nc.vector.tensor_copy(out=bias[:], in_=raw_b2[:])
+        for n in range(SIDE_LEAD):
+            regroup_side(n)
 
         for k in range(len(rounds) + 2):
             spread_scales(k + 1)
             scale_rows(k, 0)
-            quantise_messages(k)
-            if round_starts_at(k, 0):
-                column_sum_roots(rounds[k][0] + 1)
-            quantise_adjacency(k - 1, 1)
-            regroup_adjacency(k, 0)
             hidden_layer(k - 1)
+            regroup_adjacency(k, 0)
             scale_rows(k, 1)
             regroup_hidden(k - 1)
-            if k == 0:
-                quantise(w_codes[:], w_scales[:], w_grouped[:])
+            regroup_adjacency(k, 1)
+            quantise_adjacency(k, 0)
             if round_starts_at(k, 0):
                 node_scales(rounds[k][0] + 1)
             quantise_hidden(k - 2)
-            quantise_adjacency(k, 0)
-            regroup_adjacency(k, 1)
             project(k - 2)
             if round_starts_at(k, ROUND):
                 column_sums(rounds[k][0] + 2)
-            regroup_messages(k + 1, nc.scalar.copy)
+            for n in range(SIDE_PER_TURN * k, SIDE_PER_TURN * (k + 1)):
+                quantise_side(n)
+            regroup_side(SIDE_LEAD + k)
+            quantise_adjacency(k, 1)

@@ -66,6 +66,7 @@ def tile_gcn_pb_kernel(tc, adj, msg, b2, W3, out):
         stage = ctx.enter_context(tc.tile_pool(name="stage", bufs=2))
         operand = ctx.enter_context(tc.tile_pool(name="operand", bufs=2 * PASSES))
         store = ctx.enter_context(tc.tile_pool(name="store", bufs=6))
+        half_pool = ctx.enter_context(tc.tile_pool(name="half_pool", bufs=3))
         psum_sum = ctx.enter_context(tc.psum_pool(name="psum_sum", bufs=1))
         psum_r = ctx.enter_context(tc.psum_pool(name="psum_r", bufs=2))
         psum_x = ctx.enter_context(tc.psum_pool(name="psum_x", bufs=3))
@@ -124,7 +125,7 @@ def tile_gcn_pb_kernel(tc, adj, msg, b2, W3, out):
         partial = {}
         r_of = {}
         r_row = {}
-        scaled = {}
+        half = {}
         a_grouped = {}
         a_operand = {}
         x_rows = {}
@@ -193,24 +194,30 @@ def tile_gcn_pb_kernel(tc, adj, msg, b2, W3, out):
             if k >= len(rounds):
                 return
             g, first, width = rounds[k]
-            scaled[k, c] = stage.tile([P, PACK, width], BF16, name="scaled")
+            half[k, c] = half_pool.tile([P, PACK, width], F32, name="half")
             for t in range(PACK):
                 a = c * PACK + t
-                nc.vector.scalar_tensor_tensor(
-                    out=scaled[k, c][:, t, :],
+                nc.gpsimd.tensor_scalar(
+                    out=half[k, c][:, t, :],
                     in0=raw_adj[g][:, c, t, first : first + width],
-                    scalar=r_of[g][:, a : a + 1],
-                    in1=r_row[k][:],
+                    scalar1=r_of[g][:, a : a + 1],
+                    scalar2=0.0,
                     op0=ALU.mult,
-                    op1=ALU.mult,
+                    op1=ALU.add,
                 )
 
-        def regroup_adjacency(k, c):
+        def scale_columns(k, c):
             if k >= len(rounds):
                 return
             width = rounds[k][2]
             a_grouped[k, c] = stage.tile([P, width, PACK], BF16, name="a_grouped", align_bytes=64)
-            regroup(nc.vector.tensor_copy, a_grouped[k, c][:], scaled[k, c][:])
+            r_run = r_row[k][:].rearrange("p (w i) -> p w i", i=RUN).unsqueeze(2)
+            nc.vector.tensor_tensor(
+                out=a_grouped[k, c][:].rearrange("p (w i) t -> p w t i", i=RUN),
+                in0=half[k, c][:].rearrange("p t (w i) -> p w t i", i=RUN),
+                in1=r_run.to_broadcast([P, width // RUN, PACK, RUN]),
+                op=ALU.mult,
+            )
 
         def quantise_adjacency(k, c):
             if k >= len(rounds):
@@ -249,7 +256,7 @@ def tile_gcn_pb_kernel(tc, adj, msg, b2, W3, out):
                 return
             width = rounds[k][2]
             x_grouped[k] = stage.tile([P, width, PACK], BF16, name="x_grouped", align_bytes=64)
-            regroup(nc.scalar.copy, x_grouped[k][:], x_rows[k][:])
+            regroup(nc.vector.tensor_copy, x_grouped[k][:], x_rows[k][:])
 
         def quantise_hidden(k):
             if not 0 <= k < len(rounds):
@@ -290,22 +297,24 @@ def tile_gcn_pb_kernel(tc, adj, msg, b2, W3, out):
         for n in range(SIDE_LEAD):
             regroup_side(n)
 
+        scale_rows(0, 0)
+        scale_rows(0, 1)
         for k in range(len(rounds) + 2):
-            spread_scales(k + 1)
-            scale_rows(k, 0)
-            hidden_layer(k - 1)
-            regroup_adjacency(k, 0)
-            scale_rows(k, 1)
-            regroup_hidden(k - 1)
-            regroup_adjacency(k, 1)
-            quantise_adjacency(k, 0)
-            if round_starts_at(k, 0):
+            if round_starts_at(k, ROUND):
                 node_scales(rounds[k][0] + 1)
+            scale_rows(k + 1, 0)
+            scale_rows(k + 1, 1)
+            scale_columns(k, 0)
+            hidden_layer(k - 1)
             quantise_hidden(k - 2)
             project(k - 2)
+            spread_scales(k + 1)
+            scale_columns(k, 1)
+            quantise_adjacency(k, 0)
             if round_starts_at(k, ROUND):
                 column_sums(rounds[k][0] + 2)
             for n in range(SIDE_PER_TURN * k, SIDE_PER_TURN * (k + 1)):
                 quantise_side(n)
             regroup_side(SIDE_LEAD + k)
+            regroup_hidden(k - 1)
             quantise_adjacency(k, 1)

@@ -197,14 +197,14 @@ def tile_gcn_pb_kernel(tc, adj, msg, b2, W3, out):
             half[k, c] = half_pool.tile([P, PACK, width], F32, name="half")
             for t in range(PACK):
                 a = c * PACK + t
-                nc.gpsimd.tensor_scalar(
-                    out=half[k, c][:, t, :],
-                    in0=raw_adj[g][:, c, t, first : first + width],
-                    scalar1=r_of[g][:, a : a + 1],
-                    scalar2=0.0,
-                    op0=ALU.mult,
-                    op1=ALU.add,
-                )
+                rows = raw_adj[g][:, c, t, first : first + width]
+                r_rows = r_of[g][:, a : a + 1]
+                if c == 0:
+                    nc.gpsimd.tensor_scalar(
+                        out=half[k, c][:, t, :], in0=rows, scalar1=r_rows, scalar2=0.0, op0=ALU.mult, op1=ALU.add
+                    )
+                else:
+                    nc.scalar.activation(out=half[k, c][:, t, :], in_=rows, func=ACT.Copy, scale=r_rows)
 
         def scale_columns(k, c):
             if k >= len(rounds):
@@ -303,7 +303,6 @@ def tile_gcn_pb_kernel(tc, adj, msg, b2, W3, out):
             if round_starts_at(k, ROUND):
                 node_scales(rounds[k][0] + 1)
             scale_rows(k + 1, 0)
-            scale_rows(k + 1, 1)
             scale_columns(k, 0)
             hidden_layer(k - 1)
             quantise_hidden(k - 2)
@@ -316,5 +315,6 @@ def tile_gcn_pb_kernel(tc, adj, msg, b2, W3, out):
             for n in range(SIDE_PER_TURN * k, SIDE_PER_TURN * (k + 1)):
                 quantise_side(n)
             regroup_side(SIDE_LEAD + k)
+            scale_rows(k + 1, 1)
             regroup_hidden(k - 1)
             quantise_adjacency(k, 1)

@@ -22,8 +22,7 @@ PASSES = NODES // K_PASS
 NODE_TILES = NODES // P
 ROUND = 512
 RUN = 4
-SIDE_LEAD = 7
-SIDE_PER_TURN = 3
+SCALAR_ROW = 3
 SUM_COPIES = 8
 
 FLOPS = 2 * GRAPHS * NODES * NODES * HIDDEN + 2 * GRAPHS * NODES * HIDDEN * OUT
@@ -62,11 +61,10 @@ def tile_gcn_pb_kernel(tc, adj, msg, b2, W3, out):
         const = ctx.enter_context(tc.tile_pool(name="const", bufs=1))
         inputs = ctx.enter_context(tc.tile_pool(name="inputs", bufs=GRAPHS))
         small = ctx.enter_context(tc.tile_pool(name="small", bufs=2))
-        side_pool = ctx.enter_context(tc.tile_pool(name="side_pool", bufs=SIDE_LEAD))
+        side_pool = ctx.enter_context(tc.tile_pool(name="side_pool", bufs=2))
         stage = ctx.enter_context(tc.tile_pool(name="stage", bufs=2))
-        operand = ctx.enter_context(tc.tile_pool(name="operand", bufs=2 * PASSES))
+        operand = ctx.enter_context(tc.tile_pool(name="operand", bufs=2))
         store = ctx.enter_context(tc.tile_pool(name="store", bufs=6))
-        half_pool = ctx.enter_context(tc.tile_pool(name="half_pool", bufs=3))
         psum_sum = ctx.enter_context(tc.psum_pool(name="psum_sum", bufs=1))
         psum_r = ctx.enter_context(tc.psum_pool(name="psum_r", bufs=2))
         psum_x = ctx.enter_context(tc.psum_pool(name="psum_x", bufs=3))
@@ -74,28 +72,27 @@ def tile_gcn_pb_kernel(tc, adj, msg, b2, W3, out):
 
         ones = const.tile([P, SUM_COPIES], BF16)
         nc.vector.memset(ones[:], 1.0)
-        minus_half = const.tile([P, NODE_TILES], F32)
-        nc.vector.memset(minus_half[:], -0.5)
         identity = const.tile([P, P], F32)
         make_identity(nc, identity[:])
 
         raw_adj = {}
         raw_msg = {}
 
-        def load_adj(g):
+        def load_adj(g, pieces):
             raw_adj[g] = inputs.tile([P, PASSES, PACK, NODES], BF16, name="raw_adj")
-            rows = adj[g].rearrange("(c t p) i -> c p t i", t=PACK, p=P)
-            for c in range(PASSES):
-                nc.sync.dma_start(out=raw_adj[g][:, c], in_=rows[c])
+            flat = raw_adj[g][:].rearrange("p c t i -> p (c t) i")
+            rows = adj[g].rearrange("(a p) i -> p a i", p=P)
+            step = NODE_TILES // pieces
+            for a in range(0, NODE_TILES, step):
+                nc.sync.dma_start(out=flat[:, a : a + step, :], in_=rows[:, a : a + step, :])
 
         def load_msg(g):
             raw_msg[g] = inputs.tile([P, PASSES, PACK, HIDDEN], BF16, name="raw_msg")
-            nc.sync.dma_start(
-                out=raw_msg[g][:].rearrange("p c t f -> p (c t) f"),
-                in_=msg[g].rearrange("(a p) f -> p a f", p=P),
-            )
+            rows = msg[g].rearrange("(c t p) f -> c p t f", t=PACK, p=P)
+            for c in range(PASSES):
+                nc.sync.dma_start(out=raw_msg[g][:, c], in_=rows[c])
 
-        load_adj(0)
+        load_adj(0, 4)
         load_msg(0)
         raw_w3 = const.tile([P, PACK, OUT], BF16)
         nc.sync.dma_start(out=raw_w3[:], in_=W3.rearrange("(t p) o -> p t o", p=P))
@@ -103,26 +100,23 @@ def tile_gcn_pb_kernel(tc, adj, msg, b2, W3, out):
         with nc.allow_non_contiguous_dma(reason="512 bias values, one to a partition and word slot"):
             nc.sync.dma_start(out=raw_b2[:], in_=b2.rearrange("(t p) -> p t", p=P))
         load_msg(1)
-        load_adj(1)
+        load_adj(1, 2)
+        load_adj(2, 2)
         load_msg(2)
         load_msg(3)
-        load_adj(2)
-        load_adj(3)
+        load_adj(3, 2)
 
         w_codes = const.tile([P, OUT], U32, align_bytes=64)
         w_scales = const.tile([P, OUT], U8, align_bytes=64)
+        w_grouped = const.tile([P, OUT, PACK], BF16, align_bytes=64)
         m_codes = {}
         m_scales = {}
-        side = []
-        for g in range(GRAPHS):
-            m_codes[g] = inputs.tile([P, PASSES, HIDDEN], U32, name="m_codes", align_bytes=64)
-            m_scales[g] = inputs.tile([P, PASSES, HIDDEN], U8, name="m_scales", align_bytes=64)
-            for c in range(PASSES):
-                side.append((raw_msg[g][:, c], m_codes[g][:, c, :], m_scales[g][:, c, :]))
-            if g == 0:
-                side.append((raw_w3[:], w_codes[:], w_scales[:]))
-        side_grouped = {}
+        m_grouped = {}
         partial = {}
+        colsum = {}
+        safe = {}
+        table = {}
+        estimate = {}
         r_of = {}
         r_row = {}
         half = {}
@@ -132,48 +126,77 @@ def tile_gcn_pb_kernel(tc, adj, msg, b2, W3, out):
         x_grouped = {}
         x_operand = {}
 
-        def regroup_side(n):
-            if n < len(side):
-                side_grouped[n] = side_pool.tile([P, HIDDEN, PACK], BF16, name="side_grouped", align_bytes=64)
-                regroup(nc.scalar.copy, side_grouped[n][:], side[n][0])
-
-        def quantise_side(n):
-            if n < len(side):
-                quantise(side[n][1], side[n][2], side_grouped[n][:])
-
-        def column_sums(g):
+        def regroup_messages(copy, g, c):
             if g >= GRAPHS:
                 return
-            partial[g] = psum_sum.tile([P, NODE_TILES, NODE_TILES, SUM_COPIES], F32, name="partial")
-            for c in range(PASSES):
-                for t in range(PACK):
-                    for b in range(NODE_TILES):
-                        nc.tensor.matmul(
-                            out=partial[g][:, c * PACK + t, b, :],
-                            lhsT=raw_adj[g][:, c, t, b * P : (b + 1) * P],
-                            rhs=ones[:],
-                            start=True,
-                            stop=True,
-                        )
+            if c == 0:
+                m_grouped[g] = side_pool.tile([P, PASSES, HIDDEN, PACK], BF16, name="m_grouped", align_bytes=64)
+            regroup(copy, m_grouped[g][:, c], raw_msg[g][:, c])
 
-        def node_scales(g):
+        def quantise_messages(g):
             if g >= GRAPHS:
                 return
-            colsum = small.tile([P, NODE_TILES], F32)
+            m_codes[g] = inputs.tile([P, PASSES, HIDDEN], U32, name="m_codes", align_bytes=64)
+            m_scales[g] = inputs.tile([P, PASSES, HIDDEN], U8, name="m_scales", align_bytes=64)
+            quantise(
+                m_codes[g][:].rearrange("p c f -> p (c f)"),
+                m_scales[g][:].rearrange("p c f -> p (c f)"),
+                m_grouped[g][:].rearrange("p c f t -> p (c f) t"),
+            )
+
+        def column_sums(g, c):
+            if g >= GRAPHS:
+                return
+            if c == 0:
+                partial[g] = psum_sum.tile([P, NODE_TILES, NODE_TILES, SUM_COPIES], F32, name="partial")
+            for t in range(PACK):
+                for b in range(NODE_TILES):
+                    nc.tensor.matmul(
+                        out=partial[g][:, c * PACK + t, b, :],
+                        lhsT=raw_adj[g][:, c, t, b * P : (b + 1) * P],
+                        rhs=ones[:],
+                        start=True,
+                        stop=True,
+                    )
+
+        def look_up_scales(g):
+            if g >= GRAPHS:
+                return
+            colsum[g] = small.tile([P, NODE_TILES], F32, name="colsum")
             nc.vector.tensor_reduce(
-                out=colsum[:],
+                out=colsum[g][:],
                 in_=partial[g][:, :, :, 0].rearrange("p a b -> p b a"),
                 axis=mybir.AxisListType.X,
                 op=ALU.add,
             )
-            empty = small.tile([P, NODE_TILES], F32)
-            nc.gpsimd.tensor_single_scalar(out=empty[:], in_=colsum[:], scalar=0.0, op=ALU.is_le)
-            safe = small.tile([P, NODE_TILES], F32)
-            nc.gpsimd.tensor_tensor(out=safe[:], in0=colsum[:], in1=empty[:], op=ALU.add)
-            root = small.tile([P, NODE_TILES], F32)
-            nc.gpsimd.tensor_tensor(out=root[:], in0=safe[:], in1=minus_half[:], op=ALU.pow)
+            safe[g] = small.tile([P, NODE_TILES], F32, name="safe")
+            nc.vector.scalar_tensor_tensor(
+                out=safe[g][:], in0=colsum[g][:], scalar=0.0, in1=colsum[g][:], op0=ALU.is_le, op1=ALU.add
+            )
+            table[g] = small.tile([P, NODE_TILES], F32, name="table")
+            nc.scalar.activation(out=table[g][:], in_=safe[g][:], func=ACT.Abs_reciprocal_sqrt)
+
+        def estimate_scales(g):
+            if g >= GRAPHS:
+                return
+            estimate[g] = small.tile([P, NODE_TILES], F32, name="estimate")
+            nc.vector.scalar_tensor_tensor(
+                out=estimate[g][:], in0=colsum[g][:], scalar=0.0, in1=table[g][:], op0=ALU.is_gt, op1=ALU.mult
+            )
+
+        def refine_scales(g):
+            if g >= GRAPHS:
+                return
+            product = small.tile([P, NODE_TILES], F32)
+            nc.vector.tensor_tensor(out=product[:], in0=safe[g][:], in1=estimate[g][:], op=ALU.mult)
+            decrease = small.tile([P, NODE_TILES], F32)
+            nc.vector.scalar_tensor_tensor(
+                out=decrease[:], in0=product[:], scalar=-0.5, in1=estimate[g][:], op0=ALU.mult, op1=ALU.mult
+            )
             r_of[g] = small.tile([P, NODE_TILES], F32, name="r")
-            nc.gpsimd.tensor_tensor(out=r_of[g][:], in0=root[:], in1=empty[:], op=ALU.subtract)
+            nc.vector.scalar_tensor_tensor(
+                out=r_of[g][:], in0=decrease[:], scalar=1.5, in1=estimate[g][:], op0=ALU.add, op1=ALU.mult
+            )
 
         def spread_scales(k):
             if k >= len(rounds):
@@ -190,60 +213,74 @@ def tile_gcn_pb_kernel(tc, adj, msg, b2, W3, out):
                     stop=True,
                 )
 
-        def scale_rows(k, c):
+        def scale_rows(k):
             if k >= len(rounds):
                 return
             g, first, width = rounds[k]
-            half[k, c] = half_pool.tile([P, PACK, width], F32, name="half")
-            for t in range(PACK):
-                a = c * PACK + t
-                rows = raw_adj[g][:, c, t, first : first + width]
-                r_rows = r_of[g][:, a : a + 1]
-                if c == 0:
-                    nc.gpsimd.tensor_scalar(
-                        out=half[k, c][:, t, :], in0=rows, scalar1=r_rows, scalar2=0.0, op0=ALU.mult, op1=ALU.add
-                    )
-                else:
-                    nc.scalar.activation(out=half[k, c][:, t, :], in_=rows, func=ACT.Copy, scale=r_rows)
+            half[k] = stage.tile([P, PASSES, PACK, width], F32, name="half")
+            r_now = small.tile([P, NODE_TILES], F32, name="r_now")
+            nc.vector.tensor_copy(out=r_now[:], in_=r_of[g][:])
+            for c in range(PASSES):
+                for t in range(PACK):
+                    a = c * PACK + t
+                    rows = raw_adj[g][:, c, t, first : first + width]
+                    if t == SCALAR_ROW:
+                        nc.scalar.activation(
+                            out=half[k][:, c, t, :], in_=rows, func=ACT.Copy, scale=r_of[g][:, a : a + 1]
+                        )
+                    else:
+                        nc.gpsimd.tensor_scalar(
+                            out=half[k][:, c, t, :],
+                            in0=rows,
+                            scalar1=r_now[:, a : a + 1],
+                            scalar2=0.0,
+                            op0=ALU.mult,
+                            op1=ALU.add,
+                        )
 
         def scale_columns(k, c):
             if k >= len(rounds):
                 return
             width = rounds[k][2]
-            a_grouped[k, c] = stage.tile([P, width, PACK], BF16, name="a_grouped", align_bytes=64)
+            if c == 0:
+                a_grouped[k] = stage.tile([P, PASSES, width, PACK], BF16, name="a_grouped", align_bytes=64)
             r_run = r_row[k][:].rearrange("p (w i) -> p w i", i=RUN).unsqueeze(2)
             nc.vector.tensor_tensor(
-                out=a_grouped[k, c][:].rearrange("p (w i) t -> p w t i", i=RUN),
-                in0=half[k, c][:].rearrange("p t (w i) -> p w t i", i=RUN),
+                out=a_grouped[k][:, c].rearrange("p (w i) t -> p w t i", i=RUN),
+                in0=half[k][:, c].rearrange("p t (w i) -> p w t i", i=RUN),
                 in1=r_run.to_broadcast([P, width // RUN, PACK, RUN]),
                 op=ALU.mult,
             )
 
-        def quantise_adjacency(k, c):
+        def quantise_adjacency(k):
             if k >= len(rounds):
                 return
             width = rounds[k][2]
-            a_codes = operand.tile([P, width], U32, align_bytes=64)
-            a_scales = operand.tile([P, width], U8, align_bytes=64)
-            quantise(a_codes[:], a_scales[:], a_grouped[k, c][:])
-            a_operand[k, c] = (a_codes, a_scales)
+            a_codes = operand.tile([P, PASSES, width], U32, align_bytes=64)
+            a_scales = operand.tile([P, PASSES, width], U8, align_bytes=64)
+            quantise(
+                a_codes[:].rearrange("p c w -> p (c w)"),
+                a_scales[:].rearrange("p c w -> p (c w)"),
+                a_grouped[k][:].rearrange("p c w t -> p (c w) t"),
+            )
+            a_operand[k] = (a_codes, a_scales)
 
         def hidden_layer(k):
-            if not 0 <= k < len(rounds):
+            if k >= len(rounds):
                 return
             g, first, width = rounds[k]
             x_rows[k] = stage.tile([P, PACK, width], BF16, name="x_rows")
+            a_codes, a_scales = a_operand[k]
             for t in range(PACK):
                 features = slice(t * P, (t + 1) * P)
                 x_sum = psum_x.tile([P, width], F32)
                 for c in range(PASSES):
-                    a_codes, a_scales = a_operand[k, c]
                     nc.tensor.matmul_mx(
                         out=x_sum[:],
                         lhsT=m_codes[g][:, c, features].bitcast(FP8X4),
                         lhsT_scale=m_scales[g][:, c, features],
-                        rhs=a_codes[:].bitcast(FP8X4),
-                        rhs_scale=a_scales[:],
+                        rhs=a_codes[:, c, :].bitcast(FP8X4),
+                        rhs_scale=a_scales[:, c, :],
                         start=(c == 0),
                         stop=(c == PASSES - 1),
                     )
@@ -288,33 +325,49 @@ def tile_gcn_pb_kernel(tc, adj, msg, b2, W3, out):
                 nc.scalar.copy(out=result[:], in_=product[:])
                 nc.sync.dma_start(out=out[g, first + n * P : first + (n + 1) * P, :], in_=result[:])
 
-        column_sums(0)
-        node_scales(0)
+        column_sums(0, 0)
+        column_sums(0, 1)
+        look_up_scales(0)
+        estimate_scales(0)
+        refine_scales(0)
         spread_scales(0)
-        column_sums(1)
+        regroup_messages(nc.vector.tensor_copy, 0, 0)
+        regroup_messages(nc.vector.tensor_copy, 0, 1)
+        regroup(nc.scalar.copy, w_grouped[:], raw_w3[:])
+        scale_rows(0)
         bias = const.tile([P, PACK], F32)
         nc.vector.tensor_copy(out=bias[:], in_=raw_b2[:])
-        for n in range(SIDE_LEAD):
-            regroup_side(n)
+        column_sums(1, 0)
+        column_sums(1, 1)
+        regroup_messages(nc.scalar.copy, 1, 0)
+        regroup_messages(nc.scalar.copy, 1, 1)
+        quantise_messages(0)
+        spread_scales(1)
 
-        scale_rows(0, 0)
-        scale_rows(0, 1)
         for k in range(len(rounds) + 2):
+            scale_rows(k + 1)
+            if round_starts_at(k, 0):
+                regroup_messages(nc.scalar.copy, rounds[k][0] + 2, 0)
             if round_starts_at(k, ROUND):
-                node_scales(rounds[k][0] + 1)
-            scale_rows(k + 1, 0)
-            scale_columns(k, 0)
-            hidden_layer(k - 1)
-            quantise_hidden(k - 2)
+                regroup_messages(nc.scalar.copy, rounds[k][0] + 2, 1)
             project(k - 2)
-            spread_scales(k + 1)
+            scale_columns(k, 0)
             scale_columns(k, 1)
-            quantise_adjacency(k, 0)
-            if round_starts_at(k, ROUND):
-                column_sums(rounds[k][0] + 2)
-            for n in range(SIDE_PER_TURN * k, SIDE_PER_TURN * (k + 1)):
-                quantise_side(n)
-            regroup_side(SIDE_LEAD + k)
-            scale_rows(k + 1, 1)
+            if round_starts_at(k, 0):
+                look_up_scales(rounds[k][0] + 1)
             regroup_hidden(k - 1)
-            quantise_adjacency(k, 1)
+            quantise_adjacency(k)
+            hidden_layer(k)
+            if k == 0:
+                quantise(w_codes[:], w_scales[:], w_grouped[:])
+            if round_starts_at(k, 0):
+                quantise_messages(rounds[k][0] + 1)
+                estimate_scales(rounds[k][0] + 1)
+            quantise_hidden(k - 1)
+            if round_starts_at(k, 0):
+                refine_scales(rounds[k][0] + 1)
+            spread_scales(k + 2)
+            if round_starts_at(k, 0):
+                column_sums(rounds[k][0] + 2, 0)
+            if round_starts_at(k, ROUND):
+                column_sums(rounds[k][0] + 2, 1)

@@ -22,7 +22,8 @@ PASSES = NODES // K_PASS
 NODE_TILES = NODES // P
 ROUND = 512
 RUN = 4
-SCALAR_ROW = 3
+PAIR = 2
+SCALAR_ROWS = 1
 SUM_COPIES = 8
 
 FLOPS = 2 * GRAPHS * NODES * NODES * HIDDEN + 2 * GRAPHS * NODES * HIDDEN * OUT
@@ -33,17 +34,18 @@ def tile_gcn_pb_kernel(tc, adj, msg, b2, W3, out):
 
     rounds = []
     for g in range(GRAPHS):
-        for first in range(0, NODES, ROUND):
-            rounds.append((g, first, ROUND))
-    g, first, width = rounds.pop()
-    while width > P:
-        width //= 2
-        rounds.append((g, first, width))
-        first += width
-    rounds.append((g, first, width))
+        widths = [ROUND] * (NODES // ROUND)
+        if g == 0:
+            widths[:1] = [ROUND // 2, ROUND // 2]
+        if g == GRAPHS - 1:
+            widths[-1:] = [ROUND // 2, ROUND // 2]
+        first = 0
+        for width in widths:
+            rounds.append((g, first, width))
+            first += width
 
-    def round_starts_at(k, node):
-        return k < len(rounds) and rounds[k][1] == node
+    def ends_graph(k):
+        return 0 <= k < len(rounds) and rounds[k][1] + rounds[k][2] == NODES
 
     def regroup(copy, grouped, rows):
         copy(
@@ -101,8 +103,8 @@ def tile_gcn_pb_kernel(tc, adj, msg, b2, W3, out):
             nc.sync.dma_start(out=raw_b2[:], in_=b2.rearrange("(t p) -> p t", p=P))
         load_msg(1)
         load_adj(1, 2)
-        load_adj(2, 2)
         load_msg(2)
+        load_adj(2, 2)
         load_msg(3)
         load_adj(3, 2)
 
@@ -218,13 +220,18 @@ def tile_gcn_pb_kernel(tc, adj, msg, b2, W3, out):
                 return
             g, first, width = rounds[k]
             half[k] = stage.tile([P, PASSES, PACK, width], F32, name="half")
-            r_now = small.tile([P, NODE_TILES], F32, name="r_now")
-            nc.vector.tensor_copy(out=r_now[:], in_=r_of[g][:])
+            if k == 0:
+                by_scalar = range(PACK)
+                r_now = r_of[g]
+            else:
+                by_scalar = range(NODE_TILES - SCALAR_ROWS, NODE_TILES)
+                r_now = small.tile([P, NODE_TILES], F32, name="r_now")
+                nc.vector.tensor_copy(out=r_now[:], in_=r_of[g][:])
             for c in range(PASSES):
                 for t in range(PACK):
                     a = c * PACK + t
                     rows = raw_adj[g][:, c, t, first : first + width]
-                    if t == SCALAR_ROW:
+                    if a in by_scalar:
                         nc.scalar.activation(
                             out=half[k][:, c, t, :], in_=rows, func=ACT.Copy, scale=r_of[g][:, a : a + 1]
                         )
@@ -244,11 +251,11 @@ def tile_gcn_pb_kernel(tc, adj, msg, b2, W3, out):
             width = rounds[k][2]
             if c == 0:
                 a_grouped[k] = stage.tile([P, PASSES, width, PACK], BF16, name="a_grouped", align_bytes=64)
-            r_run = r_row[k][:].rearrange("p (w i) -> p w i", i=RUN).unsqueeze(2)
+            r_run = r_row[k][:].rearrange("p (w i) -> p w i", i=PAIR).unsqueeze(2)
             nc.vector.tensor_tensor(
-                out=a_grouped[k][:, c].rearrange("p (w i) t -> p w t i", i=RUN),
-                in0=half[k][:, c].rearrange("p t (w i) -> p w t i", i=RUN),
-                in1=r_run.to_broadcast([P, width // RUN, PACK, RUN]),
+                out=a_grouped[k][:, c].rearrange("p (w i) t -> p w t i", i=PAIR),
+                in0=half[k][:, c].rearrange("p t (w i) -> p w t i", i=PAIR),
+                in1=r_run.to_broadcast([P, width // PAIR, PACK, PAIR]),
                 op=ALU.mult,
             )
 
@@ -266,7 +273,7 @@ def tile_gcn_pb_kernel(tc, adj, msg, b2, W3, out):
             a_operand[k] = (a_codes, a_scales)
 
         def hidden_layer(k):
-            if k >= len(rounds):
+            if not 0 <= k < len(rounds):
                 return
             g, first, width = rounds[k]
             x_rows[k] = stage.tile([P, PACK, width], BF16, name="x_rows")
@@ -288,12 +295,12 @@ def tile_gcn_pb_kernel(tc, adj, msg, b2, W3, out):
                     out=x_rows[k][:, t, :], in_=x_sum[:], func=ACT.Relu, bias=bias[:, t : t + 1], scale=1.0
                 )
 
-        def regroup_hidden(k):
+        def regroup_hidden(k, copy):
             if not 0 <= k < len(rounds):
                 return
             width = rounds[k][2]
             x_grouped[k] = stage.tile([P, width, PACK], BF16, name="x_grouped", align_bytes=64)
-            regroup(nc.vector.tensor_copy, x_grouped[k][:], x_rows[k][:])
+            regroup(copy, x_grouped[k][:], x_rows[k][:])
 
         def quantise_hidden(k):
             if not 0 <= k < len(rounds):
@@ -331,43 +338,50 @@ def tile_gcn_pb_kernel(tc, adj, msg, b2, W3, out):
         estimate_scales(0)
         refine_scales(0)
         spread_scales(0)
-        regroup_messages(nc.vector.tensor_copy, 0, 0)
-        regroup_messages(nc.vector.tensor_copy, 0, 1)
-        regroup(nc.scalar.copy, w_grouped[:], raw_w3[:])
         scale_rows(0)
+        regroup_messages(nc.vector.tensor_copy, 0, 0)
         bias = const.tile([P, PACK], F32)
         nc.vector.tensor_copy(out=bias[:], in_=raw_b2[:])
-        column_sums(1, 0)
-        column_sums(1, 1)
-        regroup_messages(nc.scalar.copy, 1, 0)
-        regroup_messages(nc.scalar.copy, 1, 1)
-        quantise_messages(0)
-        spread_scales(1)
+        regroup_messages(nc.scalar.copy, 0, 1)
 
         for k in range(len(rounds) + 2):
+            graph = rounds[k][0] if k < len(rounds) else GRAPHS
             scale_rows(k + 1)
-            if round_starts_at(k, 0):
-                regroup_messages(nc.scalar.copy, rounds[k][0] + 2, 0)
-            if round_starts_at(k, ROUND):
-                regroup_messages(nc.scalar.copy, rounds[k][0] + 2, 1)
-            project(k - 2)
+            hidden_layer(k - 1)
+            scalar_regroups = ends_graph(k - 1) and k < len(rounds)
+            if scalar_regroups:
+                regroup_hidden(k - 1, nc.scalar.copy)
+            spread_scales(k + 1)
             scale_columns(k, 0)
-            scale_columns(k, 1)
-            if round_starts_at(k, 0):
-                look_up_scales(rounds[k][0] + 1)
-            regroup_hidden(k - 1)
-            quantise_adjacency(k)
-            hidden_layer(k)
             if k == 0:
+                regroup(nc.scalar.copy, w_grouped[:], raw_w3[:])
+                column_sums(1, 0)
+                column_sums(1, 1)
+            if ends_graph(k + 1):
+                look_up_scales(graph + 1)
+            if k == 0:
+                regroup_messages(nc.scalar.copy, 1, 0)
+            if k == 1:
+                regroup_messages(nc.scalar.copy, 1, 1)
+            scale_columns(k, 1)
+            if ends_graph(k + 1):
+                regroup_messages(nc.scalar.copy, graph + 2, 0)
+                column_sums(graph + 2, 0)
+            if ends_graph(k):
+                regroup_messages(nc.scalar.copy, graph + 2, 1)
+                column_sums(graph + 2, 1)
+            project(k - 2)
+            if not scalar_regroups:
+                regroup_hidden(k - 1, nc.vector.tensor_copy)
+            if k == 0:
+                quantise_messages(0)
+            quantise_adjacency(k)
+            if k == 1:
                 quantise(w_codes[:], w_scales[:], w_grouped[:])
-            if round_starts_at(k, 0):
-                quantise_messages(rounds[k][0] + 1)
-                estimate_scales(rounds[k][0] + 1)
+            if ends_graph(k):
+                quantise_messages(graph + 1)
+            if ends_graph(k + 1):
+                estimate_scales(graph + 1)
             quantise_hidden(k - 1)
-            if round_starts_at(k, 0):
-                refine_scales(rounds[k][0] + 1)
-            spread_scales(k + 2)
-            if round_starts_at(k, 0):
-                column_sums(rounds[k][0] + 2, 0)
-            if round_starts_at(k, ROUND):
-                column_sums(rounds[k][0] + 2, 1)
+            if ends_graph(k + 1):
+                refine_scales(graph + 1)

@@ -22,7 +22,6 @@ PASSES = NODES // K_PASS
 NODE_TILES = NODES // P
 ROUND = 512
 RUN = 4
-PAIR = 2
 SCALAR_ROWS = 1
 SUM_COPIES = 8
 
@@ -251,11 +250,11 @@ def tile_gcn_pb_kernel(tc, adj, msg, b2, W3, out):
             width = rounds[k][2]
             if c == 0:
                 a_grouped[k] = stage.tile([P, PASSES, width, PACK], BF16, name="a_grouped", align_bytes=64)
-            r_run = r_row[k][:].rearrange("p (w i) -> p w i", i=PAIR).unsqueeze(2)
+            r_run = r_row[k][:].rearrange("p (w i) -> p w i", i=RUN).unsqueeze(2)
             nc.vector.tensor_tensor(
-                out=a_grouped[k][:, c].rearrange("p (w i) t -> p w t i", i=PAIR),
-                in0=half[k][:, c].rearrange("p t (w i) -> p w t i", i=PAIR),
-                in1=r_run.to_broadcast([P, width // PAIR, PACK, PAIR]),
+                out=a_grouped[k][:, c].rearrange("p (w i) t -> p w t i", i=RUN),
+                in0=half[k][:, c].rearrange("p t (w i) -> p w t i", i=RUN),
+                in1=r_run.to_broadcast([P, width // RUN, PACK, RUN]),
                 op=ALU.mult,
             )
 

@@ -22,6 +22,7 @@ PASSES = NODES // K_PASS
 NODE_TILES = NODES // P
 ROUND = 512
 RUN = 4
+COPY_RUN = 8
 SCALAR_ROWS = 1
 SUM_COPIES = 8
 
@@ -48,8 +49,8 @@ def tile_gcn_pb_kernel(tc, adj, msg, b2, W3, out):
 
     def regroup(copy, grouped, rows):
         copy(
-            out=grouped.rearrange("p (w i) t -> p w t i", i=RUN),
-            in_=rows.rearrange("p t (w i) -> p w t i", i=RUN),
+            out=grouped.rearrange("p (w i) t -> p w t i", i=COPY_RUN),
+            in_=rows.rearrange("p t (w i) -> p w t i", i=COPY_RUN),
         )
 
     def quantise(codes, scales, grouped):

@@ -23,7 +23,8 @@ NODE_TILES = NODES // P
 ROUND = 512
 RUN = 4
 COPY_RUN = 8
-SCALAR_ROWS = 1
+SCALAR_ROWS = 2
+TINY = 2.0**-86
 SUM_COPIES = 8
 
 FLOPS = 2 * GRAPHS * NODES * NODES * HIDDEN + 2 * GRAPHS * NODES * HIDDEN * OUT
@@ -74,6 +75,8 @@ def tile_gcn_pb_kernel(tc, adj, msg, b2, W3, out):
 
         ones = const.tile([P, SUM_COPIES], BF16)
         nc.vector.memset(ones[:], 1.0)
+        tiny = const.tile([P, 1], F32)
+        nc.vector.memset(tiny[:], TINY)
         identity = const.tile([P, P], F32)
         make_identity(nc, identity[:])
 
@@ -84,9 +87,10 @@ def tile_gcn_pb_kernel(tc, adj, msg, b2, W3, out):
             raw_adj[g] = inputs.tile([P, PASSES, PACK, NODES], BF16, name="raw_adj")
             flat = raw_adj[g][:].rearrange("p c t i -> p (c t) i")
             rows = adj[g].rearrange("(a p) i -> p a i", p=P)
-            step = NODE_TILES // pieces
-            for a in range(0, NODE_TILES, step):
+            a = 0
+            for step in pieces:
                 nc.sync.dma_start(out=flat[:, a : a + step, :], in_=rows[:, a : a + step, :])
+                a += step
 
         def load_msg(g):
             raw_msg[g] = inputs.tile([P, PASSES, PACK, HIDDEN], BF16, name="raw_msg")
@@ -94,7 +98,7 @@ def tile_gcn_pb_kernel(tc, adj, msg, b2, W3, out):
             for c in range(PASSES):
                 nc.sync.dma_start(out=raw_msg[g][:, c], in_=rows[c])
 
-        load_adj(0, 4)
+        load_adj(0, (2, 2, 2, 1, 1))
         load_msg(0)
         raw_w3 = const.tile([P, PACK, OUT], BF16)
         nc.sync.dma_start(out=raw_w3[:], in_=W3.rearrange("(t p) o -> p t o", p=P))
@@ -102,11 +106,11 @@ def tile_gcn_pb_kernel(tc, adj, msg, b2, W3, out):
         with nc.allow_non_contiguous_dma(reason="512 bias values, one to a partition and word slot"):
             nc.sync.dma_start(out=raw_b2[:], in_=b2.rearrange("(t p) -> p t", p=P))
         load_msg(1)
-        load_adj(1, 2)
+        load_adj(1, (4, 4))
         load_msg(2)
-        load_adj(2, 2)
+        load_adj(2, (4, 4))
         load_msg(3)
-        load_adj(3, 2)
+        load_adj(3, (4, 4))
 
         w_codes = const.tile([P, OUT], U32, align_bytes=64)
         w_scales = const.tile([P, OUT], U8, align_bytes=64)
@@ -116,9 +120,8 @@ def tile_gcn_pb_kernel(tc, adj, msg, b2, W3, out):
         m_grouped = {}
         partial = {}
         colsum = {}
-        safe = {}
         table = {}
-        estimate = {}
+        square = {}
         r_of = {}
         r_row = {}
         half = {}
@@ -171,33 +174,23 @@ def tile_gcn_pb_kernel(tc, adj, msg, b2, W3, out):
                 axis=mybir.AxisListType.X,
                 op=ALU.add,
             )
-            safe[g] = small.tile([P, NODE_TILES], F32, name="safe")
-            nc.vector.scalar_tensor_tensor(
-                out=safe[g][:], in0=colsum[g][:], scalar=0.0, in1=colsum[g][:], op0=ALU.is_le, op1=ALU.add
-            )
             table[g] = small.tile([P, NODE_TILES], F32, name="table")
-            nc.scalar.activation(out=table[g][:], in_=safe[g][:], func=ACT.Abs_reciprocal_sqrt)
-
-        def estimate_scales(g):
-            if g >= GRAPHS:
-                return
-            estimate[g] = small.tile([P, NODE_TILES], F32, name="estimate")
-            nc.vector.scalar_tensor_tensor(
-                out=estimate[g][:], in0=colsum[g][:], scalar=0.0, in1=table[g][:], op0=ALU.is_gt, op1=ALU.mult
-            )
+            nc.scalar.activation(out=table[g][:], in_=colsum[g][:], func=ACT.Abs_reciprocal_sqrt, bias=tiny[:])
+            square[g] = small.tile([P, NODE_TILES], F32, name="square")
+            nc.scalar.activation(out=square[g][:], in_=table[g][:], func=ACT.Square)
 
         def refine_scales(g):
             if g >= GRAPHS:
                 return
-            product = small.tile([P, NODE_TILES], F32)
-            nc.vector.tensor_tensor(out=product[:], in0=safe[g][:], in1=estimate[g][:], op=ALU.mult)
-            decrease = small.tile([P, NODE_TILES], F32)
+            near_one = small.tile([P, NODE_TILES], F32)
+            nc.vector.tensor_tensor(out=near_one[:], in0=square[g][:], in1=colsum[g][:], op=ALU.mult)
+            factor = small.tile([P, NODE_TILES], F32)
             nc.vector.scalar_tensor_tensor(
-                out=decrease[:], in0=product[:], scalar=-0.5, in1=estimate[g][:], op0=ALU.mult, op1=ALU.mult
+                out=factor[:], in0=near_one[:], scalar=-5.0 / 3.0, in1=near_one[:], op0=ALU.add, op1=ALU.mult
             )
             r_of[g] = small.tile([P, NODE_TILES], F32, name="r")
             nc.vector.scalar_tensor_tensor(
-                out=r_of[g][:], in0=decrease[:], scalar=1.5, in1=estimate[g][:], op0=ALU.add, op1=ALU.mult
+                out=r_of[g][:], in0=factor[:], scalar=-1.5, in1=table[g][:], op0=ALU.mult, op1=ALU.mult
             )
 
         def spread_scales(k):
@@ -224,7 +217,8 @@ def tile_gcn_pb_kernel(tc, adj, msg, b2, W3, out):
                 by_scalar = range(PACK)
                 r_now = r_of[g]
             else:
-                by_scalar = range(NODE_TILES - SCALAR_ROWS, NODE_TILES)
+                scalar_rows = SCALAR_ROWS if rounds[k - 1][2] >= width else NODE_TILES // 2
+                by_scalar = range(NODE_TILES - scalar_rows, NODE_TILES)
                 r_now = small.tile([P, NODE_TILES], F32, name="r_now")
                 nc.vector.tensor_copy(out=r_now[:], in_=r_of[g][:])
             for c in range(PASSES):
@@ -335,7 +329,6 @@ def tile_gcn_pb_kernel(tc, adj, msg, b2, W3, out):
         column_sums(0, 0)
         column_sums(0, 1)
         look_up_scales(0)
-        estimate_scales(0)
         refine_scales(0)
         spread_scales(0)
         scale_rows(0)
@@ -348,7 +341,7 @@ def tile_gcn_pb_kernel(tc, adj, msg, b2, W3, out):
             graph = rounds[k][0] if k < len(rounds) else GRAPHS
             scale_rows(k + 1)
             hidden_layer(k - 1)
-            scalar_regroups = ends_graph(k - 1) and k < len(rounds)
+            scalar_regroups = ends_graph(k - 1) and graph == GRAPHS - 1
             if scalar_regroups:
                 regroup_hidden(k - 1, nc.scalar.copy)
             spread_scales(k + 1)
@@ -359,29 +352,28 @@ def tile_gcn_pb_kernel(tc, adj, msg, b2, W3, out):
                 column_sums(1, 1)
             if ends_graph(k + 1):
                 look_up_scales(graph + 1)
-            if k == 0:
-                regroup_messages(nc.scalar.copy, 1, 0)
-            if k == 1:
-                regroup_messages(nc.scalar.copy, 1, 1)
             scale_columns(k, 1)
+            if k == 1:
+                regroup_messages(nc.scalar.copy, 1, 0)
             if ends_graph(k + 1):
-                regroup_messages(nc.scalar.copy, graph + 2, 0)
+                regroup_messages(nc.scalar.copy, graph + 1, 1)
                 column_sums(graph + 2, 0)
             if ends_graph(k):
-                regroup_messages(nc.scalar.copy, graph + 2, 1)
+                regroup_messages(nc.scalar.copy, graph + 2, 0)
                 column_sums(graph + 2, 1)
             project(k - 2)
+            if k >= len(rounds) - 2:
+                quantise_adjacency(k)
             if not scalar_regroups:
                 regroup_hidden(k - 1, nc.vector.tensor_copy)
             if k == 0:
                 quantise_messages(0)
-            quantise_adjacency(k)
+            if k < len(rounds) - 2:
+                quantise_adjacency(k)
             if k == 1:
                 quantise(w_codes[:], w_scales[:], w_grouped[:])
             if ends_graph(k):
                 quantise_messages(graph + 1)
             if ends_graph(k + 1):
-                estimate_scales(graph + 1)
-            quantise_hidden(k - 1)
-            if ends_graph(k + 1):
                 refine_scales(graph + 1)
+            quantise_hidden(k - 1)

@@ -23,6 +23,7 @@ NODE_TILES = NODES // P
 ROUND = 512
 RUN = 4
 COPY_RUN = 8
+VECTOR_ROWS = 1
 SCALAR_ROWS = 2
 TINY = 2.0**-86
 SUM_COPIES = 8
@@ -215,10 +216,12 @@ def tile_gcn_pb_kernel(tc, adj, msg, b2, W3, out):
             half[k] = stage.tile([P, PASSES, PACK, width], F32, name="half")
             if k == 0:
                 by_scalar = range(PACK)
+                by_vector = range(0)
                 r_now = r_of[g]
             else:
-                scalar_rows = SCALAR_ROWS if rounds[k - 1][2] >= width else NODE_TILES // 2
-                by_scalar = range(NODE_TILES - scalar_rows, NODE_TILES)
+                by_vector = range(NODE_TILES - VECTOR_ROWS, NODE_TILES)
+                scalar_rows = SCALAR_ROWS if rounds[k - 1][2] >= width else SCALAR_ROWS + 1
+                by_scalar = range(NODE_TILES - VECTOR_ROWS - scalar_rows, NODE_TILES - VECTOR_ROWS)
                 r_now = small.tile([P, NODE_TILES], F32, name="r_now")
                 nc.vector.tensor_copy(out=r_now[:], in_=r_of[g][:])
             for c in range(PASSES):
@@ -229,7 +232,7 @@ def tile_gcn_pb_kernel(tc, adj, msg, b2, W3, out):
                         nc.scalar.activation(
                             out=half[k][:, c, t, :], in_=rows, func=ACT.Copy, scale=r_of[g][:, a : a + 1]
                         )
-                    else:
+                    elif a not in by_vector:
                         nc.gpsimd.tensor_scalar(
                             out=half[k][:, c, t, :],
                             in0=rows,
@@ -238,6 +241,19 @@ def tile_gcn_pb_kernel(tc, adj, msg, b2, W3, out):
                             op0=ALU.mult,
                             op1=ALU.add,
                         )
+
+        def scale_last_rows(k):
+            if k >= len(rounds):
+                return
+            g, first, width = rounds[k]
+            for a in range(NODE_TILES - VECTOR_ROWS, NODE_TILES):
+                nc.vector.tensor_scalar(
+                    out=half[k][:, a // PACK, a % PACK, :],
+                    in0=raw_adj[g][:, a // PACK, a % PACK, first : first + width],
+                    scalar1=r_of[g][:, a : a + 1],
+                    scalar2=None,
+                    op0=ALU.mult,
+                )
 
         def scale_columns(k, c):
             if k >= len(rounds):
@@ -377,3 +393,4 @@ def tile_gcn_pb_kernel(tc, adj, msg, b2, W3, out):
             if ends_graph(k + 1):
                 refine_scales(graph + 1)
             quantise_hidden(k - 1)
+            scale_last_rows(k + 1)

@@ -103,15 +103,15 @@ def tile_gcn_pb_kernel(tc, adj, msg, b2, W3, out):
         load_msg(0)
         raw_w3 = const.tile([P, PACK, OUT], BF16)
         nc.sync.dma_start(out=raw_w3[:], in_=W3.rearrange("(t p) o -> p t o", p=P))
+        load_adj(1, (4, 4))
         raw_b2 = const.tile([P, PACK], BF16)
         with nc.allow_non_contiguous_dma(reason="512 bias values, one to a partition and word slot"):
             nc.sync.dma_start(out=raw_b2[:], in_=b2.rearrange("(t p) -> p t", p=P))
         load_msg(1)
-        load_adj(1, (4, 4))
-        load_msg(2)
         load_adj(2, (4, 4))
-        load_msg(3)
+        load_msg(2)
         load_adj(3, (4, 4))
+        load_msg(3)
 
         w_codes = const.tile([P, OUT], U32, align_bytes=64)
         w_scales = const.tile([P, OUT], U8, align_bytes=64)
@@ -288,6 +288,7 @@ def tile_gcn_pb_kernel(tc, adj, msg, b2, W3, out):
             g, first, width = rounds[k]
             x_rows[k] = stage.tile([P, PACK, width], BF16, name="x_rows")
             a_codes, a_scales = a_operand[k]
+            last = k == len(rounds) - 1
             for t in range(PACK):
                 features = slice(t * P, (t + 1) * P)
                 x_sum = psum_x.tile([P, width], F32)
@@ -301,9 +302,19 @@ def tile_gcn_pb_kernel(tc, adj, msg, b2, W3, out):
                         start=(c == 0),
                         stop=(c == PASSES - 1),
                     )
-                nc.scalar.activation(
-                    out=x_rows[k][:, t, :], in_=x_sum[:], func=ACT.Relu, bias=bias[:, t : t + 1], scale=1.0
-                )
+                if last and t % 2 == 1:
+                    nc.vector.tensor_scalar(
+                        out=x_rows[k][:, t, :],
+                        in0=x_sum[:],
+                        scalar1=raw_b2[:, t : t + 1],
+                        scalar2=0.0,
+                        op0=ALU.add,
+                        op1=ALU.max,
+                    )
+                else:
+                    nc.scalar.activation(
+                        out=x_rows[k][:, t, :], in_=x_sum[:], func=ACT.Relu, bias=raw_b2[:, t : t + 1], scale=1.0
+                    )
 
         def regroup_hidden(k, copy):
             if not 0 <= k < len(rounds):
@@ -339,25 +350,27 @@ def tile_gcn_pb_kernel(tc, adj, msg, b2, W3, out):
                     stop=True,
                 )
                 result = store.tile([P, OUT], F32)
-                nc.scalar.copy(out=result[:], in_=product[:])
+                if k == len(rounds) - 1 and n % 2 == 1:
+                    nc.vector.tensor_copy(out=result[:], in_=product[:])
+                else:
+                    nc.scalar.copy(out=result[:], in_=product[:])
                 nc.sync.dma_start(out=out[g, first + n * P : first + (n + 1) * P, :], in_=result[:])
 
         column_sums(0, 0)
         column_sums(0, 1)
         look_up_scales(0)
+        regroup_messages(nc.vector.tensor_copy, 0, 0)
         refine_scales(0)
         spread_scales(0)
         scale_rows(0)
-        regroup_messages(nc.vector.tensor_copy, 0, 0)
-        bias = const.tile([P, PACK], F32)
-        nc.vector.tensor_copy(out=bias[:], in_=raw_b2[:])
-        regroup_messages(nc.scalar.copy, 0, 1)
+        regroup_messages(nc.vector.tensor_copy, 0, 1)
+        quantise_messages(0)
 
         for k in range(len(rounds) + 2):
             graph = rounds[k][0] if k < len(rounds) else GRAPHS
             scale_rows(k + 1)
             hidden_layer(k - 1)
-            scalar_regroups = ends_graph(k - 1) and graph == GRAPHS - 1
+            scalar_regroups = ends_graph(k) and graph == GRAPHS - 2
             if scalar_regroups:
                 regroup_hidden(k - 1, nc.scalar.copy)
             spread_scales(k + 1)
@@ -382,8 +395,6 @@ def tile_gcn_pb_kernel(tc, adj, msg, b2, W3, out):
                 quantise_adjacency(k)
             if not scalar_regroups:
                 regroup_hidden(k - 1, nc.vector.tensor_copy)
-            if k == 0:
-                quantise_messages(0)
             if k < len(rounds) - 2:
                 quantise_adjacency(k)
             if k == 1:

from contextlib import ExitStack

import concourse.mybir as mybir
from concourse.masks import make_identity

BF16 = mybir.dt.bfloat16
F32 = mybir.dt.float32
U32 = mybir.dt.uint32
U8 = mybir.dt.uint8
FP8X4 = mybir.dt.float8_e4m3fn_x4
ALU = mybir.AluOpType
ACT = mybir.ActivationFunctionType

GRAPHS = 4
NODES = 1024
HIDDEN = 512
OUT = 512
P = 128
PACK = 4
K_PASS = P * PACK
PASSES = NODES // K_PASS
NODE_TILES = NODES // P
ROUND = 512
RUN = 4
COPY_RUN = 8
VECTOR_ROWS = 1
SCALAR_ROWS = 2
TINY = 2.0**-86
SUM_COPIES = 8

FLOPS = 2 * GRAPHS * NODES * NODES * HIDDEN + 2 * GRAPHS * NODES * HIDDEN * OUT


def tile_gcn_pb_kernel(tc, adj, msg, b2, W3, out):
    nc = tc.nc

    rounds = []
    for g in range(GRAPHS):
        widths = [ROUND] * (NODES // ROUND)
        if g == 0:
            widths[:1] = [ROUND // 2, ROUND // 2]
        if g == GRAPHS - 1:
            widths[-1:] = [ROUND // 2, ROUND // 2]
        first = 0
        for width in widths:
            rounds.append((g, first, width))
            first += width

    def ends_graph(k):
        return 0 <= k < len(rounds) and rounds[k][1] + rounds[k][2] == NODES

    def regroup(copy, grouped, rows):
        copy(
            out=grouped.rearrange("p (w i) t -> p w t i", i=COPY_RUN),
            in_=rows.rearrange("p t (w i) -> p w t i", i=COPY_RUN),
        )

    def quantise(codes, scales, grouped):
        nc.vector.quantize_mx(
            out=codes.bitcast(FP8X4), scales=scales, in_=grouped.rearrange("p w t -> p (w t)")
        )

    with ExitStack() as ctx:
        ctx.enter_context(tc.manual_schedule())
        const = ctx.enter_context(tc.tile_pool(name="const", bufs=1))
        inputs = ctx.enter_context(tc.tile_pool(name="inputs", bufs=GRAPHS))
        small = ctx.enter_context(tc.tile_pool(name="small", bufs=2))
        side_pool = ctx.enter_context(tc.tile_pool(name="side_pool", bufs=2))
        stage = ctx.enter_context(tc.tile_pool(name="stage", bufs=2))
        operand = ctx.enter_context(tc.tile_pool(name="operand", bufs=2))
        store = ctx.enter_context(tc.tile_pool(name="store", bufs=6))
        psum_sum = ctx.enter_context(tc.psum_pool(name="psum_sum", bufs=1))
        psum_r = ctx.enter_context(tc.psum_pool(name="psum_r", bufs=2))
        psum_x = ctx.enter_context(tc.psum_pool(name="psum_x", bufs=3))
        psum_out = ctx.enter_context(tc.psum_pool(name="psum_out", bufs=2))

        ones = const.tile([P, SUM_COPIES], BF16)
        nc.vector.memset(ones[:], 1.0)
        tiny = const.tile([P, 1], F32)
        nc.vector.memset(tiny[:], TINY)
        identity = const.tile([P, P], F32)
        make_identity(nc, identity[:])

        raw_adj = {}
        raw_msg = {}

        def load_adj(g, pieces):
            raw_adj[g] = inputs.tile([P, PASSES, PACK, NODES], BF16, name="raw_adj")
            flat = raw_adj[g][:].rearrange("p c t i -> p (c t) i")
            rows = adj[g].rearrange("(a p) i -> p a i", p=P)
            a = 0
            for step in pieces:
                nc.sync.dma_start(out=flat[:, a : a + step, :], in_=rows[:, a : a + step, :])
                a += step

        def load_msg(g):
            raw_msg[g] = inputs.tile([P, PASSES, PACK, HIDDEN], BF16, name="raw_msg")
            rows = msg[g].rearrange("(c t p) f -> c p t f", t=PACK, p=P)
            for c in range(PASSES):
                nc.sync.dma_start(out=raw_msg[g][:, c], in_=rows[c])

        load_adj(0, (2, 2, 2, 1, 1))
        load_msg(0)
        raw_w3 = const.tile([P, PACK, OUT], BF16)
        nc.sync.dma_start(out=raw_w3[:], in_=W3.rearrange("(t p) o -> p t o", p=P))
        load_adj(1, (4, 4))
        raw_b2 = const.tile([P, PACK], BF16)
        with nc.allow_non_contiguous_dma(reason="512 bias values, one to a partition and word slot"):
            nc.sync.dma_start(out=raw_b2[:], in_=b2.rearrange("(t p) -> p t", p=P))
        load_msg(1)
        load_adj(2, (4, 4))
        load_msg(2)
        load_adj(3, (4, 4))
        load_msg(3)

        w_codes = const.tile([P, OUT], U32, align_bytes=64)
        w_scales = const.tile([P, OUT], U8, align_bytes=64)
        w_grouped = const.tile([P, OUT, PACK], BF16, align_bytes=64)
        m_codes = {}
        m_scales = {}
        m_grouped = {}
        partial = {}
        colsum = {}
        table = {}
        square = {}
        r_of = {}
        r_row = {}
        half = {}
        a_grouped = {}
        a_operand = {}
        x_rows = {}
        x_grouped = {}
        x_operand = {}

        def regroup_messages(copy, g, c):
            if g >= GRAPHS:
                return
            if c == 0:
                m_grouped[g] = side_pool.tile([P, PASSES, HIDDEN, PACK], BF16, name="m_grouped", align_bytes=64)
            regroup(copy, m_grouped[g][:, c], raw_msg[g][:, c])

        def quantise_messages(g):
            if g >= GRAPHS:
                return
            m_codes[g] = inputs.tile([P, PASSES, HIDDEN], U32, name="m_codes", align_bytes=64)
            m_scales[g] = inputs.tile([P, PASSES, HIDDEN], U8, name="m_scales", align_bytes=64)
            quantise(
                m_codes[g][:].rearrange("p c f -> p (c f)"),
                m_scales[g][:].rearrange("p c f -> p (c f)"),
                m_grouped[g][:].rearrange("p c f t -> p (c f) t"),
            )

        def column_sums(g, c):
            if g >= GRAPHS:
                return
            if c == 0:
                partial[g] = psum_sum.tile([P, NODE_TILES, NODE_TILES, SUM_COPIES], F32, name="partial")
            for t in range(PACK):
                for b in range(NODE_TILES):
                    nc.tensor.matmul(
                        out=partial[g][:, c * PACK + t, b, :],
                        lhsT=raw_adj[g][:, c, t, b * P : (b + 1) * P],
                        rhs=ones[:],
                        start=True,
                        stop=True,
                    )

        def look_up_scales(g):
            if g >= GRAPHS:
                return
            colsum[g] = small.tile([P, NODE_TILES], F32, name="colsum")
            nc.vector.tensor_reduce(
                out=colsum[g][:],
                in_=partial[g][:, :, :, 0].rearrange("p a b -> p b a"),
                axis=mybir.AxisListType.X,
                op=ALU.add,
            )
            table[g] = small.tile([P, NODE_TILES], F32, name="table")
            nc.scalar.activation(out=table[g][:], in_=colsum[g][:], func=ACT.Abs_reciprocal_sqrt, bias=tiny[:])
            square[g] = small.tile([P, NODE_TILES], F32, name="square")
            nc.scalar.activation(out=square[g][:], in_=table[g][:], func=ACT.Square)

        def refine_scales(g):
            if g >= GRAPHS:
                return
            near_one = small.tile([P, NODE_TILES], F32)
            nc.vector.tensor_tensor(out=near_one[:], in0=square[g][:], in1=colsum[g][:], op=ALU.mult)
            factor = small.tile([P, NODE_TILES], F32)
            nc.vector.scalar_tensor_tensor(
                out=factor[:], in0=near_one[:], scalar=-5.0 / 3.0, in1=near_one[:], op0=ALU.add, op1=ALU.mult
            )
            r_of[g] = small.tile([P, NODE_TILES], F32, name="r")
            nc.vector.scalar_tensor_tensor(
                out=r_of[g][:], in0=factor[:], scalar=-1.5, in1=table[g][:], op0=ALU.mult, op1=ALU.mult
            )

        def spread_scales(k):
            if k >= len(rounds):
                return
            g, first, width = rounds[k]
            r_row[k] = psum_r.tile([P, width], F32, name="r_row")
            for q in range(width // P):
                b = first // P + q
                nc.tensor.matmul(
                    out=r_row[k][:, q * P : (q + 1) * P],
                    lhsT=r_of[g][:, b : b + 1].to_broadcast([P, P]),
                    rhs=identity[:],
                    start=True,
                    stop=True,
                )

        def scale_rows(k):
            if k >= len(rounds):
                return
            g, first, width = rounds[k]
            half[k] = stage.tile([P, PASSES, PACK, width], F32, name="half")
            if k == 0:
                by_scalar = range(PACK)
                by_vector = range(0)
                r_now = r_of[g]
            else:
                by_vector = range(NODE_TILES - VECTOR_ROWS, NODE_TILES)
                scalar_rows = SCALAR_ROWS if rounds[k - 1][2] >= width else SCALAR_ROWS + 1
                by_scalar = range(NODE_TILES - VECTOR_ROWS - scalar_rows, NODE_TILES - VECTOR_ROWS)
                r_now = small.tile([P, NODE_TILES], F32, name="r_now")
                nc.vector.tensor_copy(out=r_now[:], in_=r_of[g][:])
            for c in range(PASSES):
                for t in range(PACK):
                    a = c * PACK + t
                    rows = raw_adj[g][:, c, t, first : first + width]
                    if a in by_scalar:
                        nc.scalar.activation(
                            out=half[k][:, c, t, :], in_=rows, func=ACT.Copy, scale=r_of[g][:, a : a + 1]
                        )
                    elif a not in by_vector:
                        nc.gpsimd.tensor_scalar(
                            out=half[k][:, c, t, :],
                            in0=rows,
                            scalar1=r_now[:, a : a + 1],
                            scalar2=0.0,
                            op0=ALU.mult,
                            op1=ALU.add,
                        )

        def scale_last_rows(k):
            if k >= len(rounds):
                return
            g, first, width = rounds[k]
            for a in range(NODE_TILES - VECTOR_ROWS, NODE_TILES):
                nc.vector.tensor_scalar(
                    out=half[k][:, a // PACK, a % PACK, :],
                    in0=raw_adj[g][:, a // PACK, a % PACK, first : first + width],
                    scalar1=r_of[g][:, a : a + 1],
                    scalar2=None,
                    op0=ALU.mult,
                )

        def scale_columns(k, c):
            if k >= len(rounds):
                return
            width = rounds[k][2]
            if c == 0:
                a_grouped[k] = stage.tile([P, PASSES, width, PACK], BF16, name="a_grouped", align_bytes=64)
            r_run = r_row[k][:].rearrange("p (w i) -> p w i", i=RUN).unsqueeze(2)
            nc.vector.tensor_tensor(
                out=a_grouped[k][:, c].rearrange("p (w i) t -> p w t i", i=RUN),
                in0=half[k][:, c].rearrange("p t (w i) -> p w t i", i=RUN),
                in1=r_run.to_broadcast([P, width // RUN, PACK, RUN]),
                op=ALU.mult,
            )

        def quantise_adjacency(k):
            if k >= len(rounds):
                return
            width = rounds[k][2]
            a_codes = operand.tile([P, PASSES, width], U32, align_bytes=64)
            a_scales = operand.tile([P, PASSES, width], U8, align_bytes=64)
            quantise(
                a_codes[:].rearrange("p c w -> p (c w)"),
                a_scales[:].rearrange("p c w -> p (c w)"),
                a_grouped[k][:].rearrange("p c w t -> p (c w) t"),
            )
            a_operand[k] = (a_codes, a_scales)

        def hidden_layer(k):
            if not 0 <= k < len(rounds):
                return
            g, first, width = rounds[k]
            x_rows[k] = stage.tile([P, PACK, width], BF16, name="x_rows")
            a_codes, a_scales = a_operand[k]
            last = k == len(rounds) - 1
            for t in range(PACK):
                features = slice(t * P, (t + 1) * P)
                x_sum = psum_x.tile([P, width], F32)
                for c in range(PASSES):
                    nc.tensor.matmul_mx(
                        out=x_sum[:],
                        lhsT=m_codes[g][:, c, features].bitcast(FP8X4),
                        lhsT_scale=m_scales[g][:, c, features],
                        rhs=a_codes[:, c, :].bitcast(FP8X4),
                        rhs_scale=a_scales[:, c, :],
                        start=(c == 0),
                        stop=(c == PASSES - 1),
                    )
                if last and t % 2 == 1:
                    nc.vector.tensor_scalar(
                        out=x_rows[k][:, t, :],
                        in0=x_sum[:],
                        scalar1=raw_b2[:, t : t + 1],
                        scalar2=0.0,
                        op0=ALU.add,
                        op1=ALU.max,
                    )
                else:
                    nc.scalar.activation(
                        out=x_rows[k][:, t, :], in_=x_sum[:], func=ACT.Relu, bias=raw_b2[:, t : t + 1], scale=1.0
                    )

        def regroup_hidden(k, copy):
            if not 0 <= k < len(rounds):
                return
            width = rounds[k][2]
            x_grouped[k] = stage.tile([P, width, PACK], BF16, name="x_grouped", align_bytes=64)
            regroup(copy, x_grouped[k][:], x_rows[k][:])

        def quantise_hidden(k):
            if not 0 <= k < len(rounds):
                return
            width = rounds[k][2]
            x_codes = operand.tile([P, width], U32, align_bytes=64)
            x_scales = operand.tile([P, width], U8, align_bytes=64)
            quantise(x_codes[:], x_scales[:], x_grouped[k][:])
            x_operand[k] = (x_codes, x_scales)

        def project(k):
            if not 0 <= k < len(rounds):
                return
            g, first, width = rounds[k]
            x_codes, x_scales = x_operand[k]
            for n in range(width // P):
                nodes = slice(n * P, (n + 1) * P)
                product = psum_out.tile([P, OUT], F32)
                nc.tensor.matmul_mx(
                    out=product[:],
                    lhsT=x_codes[:, nodes].bitcast(FP8X4),
                    lhsT_scale=x_scales[:, nodes],
                    rhs=w_codes[:].bitcast(FP8X4),
                    rhs_scale=w_scales[:],
                    start=True,
                    stop=True,
                )
                result = store.tile([P, OUT], F32)
                if k == len(rounds) - 1 and n % 2 == 1:
                    nc.vector.tensor_copy(out=result[:], in_=product[:])
                else:
                    nc.scalar.copy(out=result[:], in_=product[:])
                nc.sync.dma_start(out=out[g, first + n * P : first + (n + 1) * P, :], in_=result[:])

        column_sums(0, 0)
        column_sums(0, 1)
        look_up_scales(0)
        regroup_messages(nc.vector.tensor_copy, 0, 0)
        refine_scales(0)
        spread_scales(0)
        scale_rows(0)
        regroup_messages(nc.vector.tensor_copy, 0, 1)
        quantise_messages(0)

        for k in range(len(rounds) + 2):
            graph = rounds[k][0] if k < len(rounds) else GRAPHS
            scale_rows(k + 1)
            hidden_layer(k - 1)
            scalar_regroups = ends_graph(k) and graph == GRAPHS - 2
            if scalar_regroups:
                regroup_hidden(k - 1, nc.scalar.copy)
            spread_scales(k + 1)
            scale_columns(k, 0)
            if k == 0:
                regroup(nc.scalar.copy, w_grouped[:], raw_w3[:])
                column_sums(1, 0)
                column_sums(1, 1)
            if ends_graph(k + 1):
                look_up_scales(graph + 1)
            scale_columns(k, 1)
            if k == 1:
                regroup_messages(nc.scalar.copy, 1, 0)
            if ends_graph(k + 1):
                regroup_messages(nc.scalar.copy, graph + 1, 1)
                column_sums(graph + 2, 0)
            if ends_graph(k):
                regroup_messages(nc.scalar.copy, graph + 2, 0)
                column_sums(graph + 2, 1)
            project(k - 2)
            if k >= len(rounds) - 2:
                quantise_adjacency(k)
            if not scalar_regroups:
                regroup_hidden(k - 1, nc.vector.tensor_copy)
            if k < len(rounds) - 2:
                quantise_adjacency(k)
            if k == 1:
                quantise(w_codes[:], w_scales[:], w_grouped[:])
            if ends_graph(k):
                quantise_messages(graph + 1)
            if ends_graph(k + 1):
                refine_scales(graph + 1)
            quantise_hidden(k - 1)
            scale_last_rows(k + 1)
